import numpy as np
import ml_dtypes


def mxq(x, axis, fmt="e4m3"):
    dtype, down = {"e4m3": (ml_dtypes.float8_e4m3fn, 7), "e5m2": (ml_dtypes.float8_e5m2, 14)}[fmt]
    v = np.moveaxis(np.asarray(x, np.float32).astype(ml_dtypes.bfloat16).astype(np.float64), axis, -1)
    blocks = v.reshape(v.shape[:-1] + (-1, 32))
    amax = np.abs(blocks).max(-1, keepdims=True)
    byte = np.maximum(np.where(amax > 0, np.frexp(amax)[1] - 1 + 127, 0) - down, 1)
    scale = np.exp2(byte - 127.0)
    codes = (blocks / scale).astype(np.float32).astype(dtype).astype(np.float64)
    return np.moveaxis((codes * scale).reshape(v.shape), -1, axis)


WIDE = False


def mx_kscale(k):
    if not WIDE:
        return np.ones(k)
    levels = np.array([10, -10, 5, -5, 0])
    a = np.random.permutation(np.resize(levels, k // 512 * 4)).reshape(k // 512, 4)
    idx = np.arange(k)
    return np.exp2(a[idx // 512, idx % 128 // 32])


BF16 = ml_dtypes.bfloat16


def bf(x):
    return np.asarray(x, np.float32).astype(BF16)


def f64(x):
    return np.asarray(x).astype(np.float64)


N, D, M, P = 4096, 8, 1024, 1024


def setup_inputs():
    a = np.log2(mx_kscale(M))
    a = a.max() - a
    x = np.random.standard_normal((N, D))
    z = np.random.uniform(0.0, 1.0, (M, D))
    z[:, 0] += a * np.log(2.0)
    g = np.random.standard_normal((M, P)) * 3.2 / np.sqrt(M)
    c = np.triu(g) + 0.25 * np.tril(g, -1) + np.eye(M, P)
    return {"x": bf(x), "design_points": bf(z), "chol_inv": bf(c * np.exp2(a)[:, None])}


def reference(x, design_points, chol_inv):
    x = f64(x)
    z = f64(design_points)
    mn = np.min(x, axis=0, keepdims=True)
    mx = np.max(x, axis=0, keepdims=True)
    xs = (x - mn) / (mx - mn)
    l1 = np.zeros((x.shape[0], z.shape[0]))
    for d in range(D):
        l1 = l1 + np.abs(xs[:, d][:, None] - z[:, d][None, :])
    k_star = np.exp(-l1)
    return mxq(k_star, 1, "e4m3") @ mxq(f64(chol_inv), 0, "e4m3")

@@ -1,0 +1,330 @@
+from contextlib import ExitStack
+
+import concourse.mybir as mybir
+from concourse.masks import make_identity
+
+F32 = mybir.dt.float32
+BF16 = mybir.dt.bfloat16
+U32 = mybir.dt.uint32
+U8 = mybir.dt.uint8
+FP8X4 = mybir.dt.float8_e4m3fn_x4
+ALU = mybir.AluOpType
+ACTF = mybir.ActivationFunctionType
+AX = mybir.AxisListType
+
+P = 128
+N_ROWS = 4096
+D = 8
+M = 1024
+COLS = 1024
+NT = N_ROWS // P
+PACK = 4
+PASSES = M // (P * PACK)
+HALF = 512
+FLOPS = 2 * N_ROWS * M * COLS
+
+
+def n_abs_of(j):
+    return 2 if j % 2 == 1 else 3
+
+
+def n_chain_of(j):
+    if j % 2 == 1:
+        return 4
+    return 3 if j % 6 == 0 else 2
+
+
+def tile_tmgp_sg_kernel(tc, x, design_points, chol_inv, out):
+    nc = tc.nc
+    with ExitStack() as ctx:
+        const = ctx.enter_context(tc.tile_pool(name="const", bufs=1))
+        terms_pool = ctx.enter_context(tc.tile_pool(name="terms", bufs=4))
+        work = ctx.enter_context(tc.tile_pool(name="work", bufs=3))
+        ps_l = ctx.enter_context(tc.psum_pool(name="ps_l", bufs=4))
+        ps_o = ctx.enter_context(tc.psum_pool(name="ps_o", bufs=4))
+
+        xb = const.tile([P, NT, D], BF16, name="xb")
+        nc.sync.dma_start(out=xb[:], in_=x.rearrange("(p j) d -> p j d", j=NT))
+        zb = const.tile([P, PASSES, PACK, D], BF16, name="zb")
+        nc.sync.dma_start(
+            out=zb[:],
+            in_=design_points.rearrange("(g p t) d -> p g t d", g=PASSES, t=PACK),
+        )
+        craw = const.tile([P, PASSES, PACK, COLS], BF16, name="craw")
+        c_view = chol_inv.rearrange("(g p t) c -> g p t c", g=PASSES, t=PACK)
+        for g in range(PASSES):
+            nc.sync.dma_start(out=craw[:, g], in_=c_view[g])
+
+        ident = const.tile([P, P], F32, name="ident")
+        make_identity(nc, ident[:])
+        ident_bf = const.tile([P, P], BF16, name="ident_bf")
+        make_identity(nc, ident_bf[:])
+        warm_in = const.tile([P, 1], F32, name="warm_in")
+        warm_out = const.tile([P, 1], F32, name="warm_out")
+        nc.vector.memset(warm_in[:], 0.0)
+        nc.scalar.activation(out=warm_out[:], in_=warm_in[:], func=ACTF.Exp)
+
+        stat = const.tile([P, P], F32, name="stat")
+        nc.vector.memset(stat[:], 0.0)
+        x_by_d = xb[:].rearrange("p j d -> p d j")
+        nc.vector.tensor_reduce(out=stat[:, 0:D], in_=x_by_d, axis=AX.X, op=ALU.max)
+        mn_part = const.tile([P, D], F32, name="mn_part")
+        nc.vector.tensor_reduce(out=mn_part[:], in_=x_by_d, axis=AX.X, op=ALU.min)
+        nc.vector.tensor_scalar(
+            out=stat[:, D : 2 * D], in0=mn_part[:], scalar1=-1.0, scalar2=None, op0=ALU.mult
+        )
+        stat_t = ps_l.tile([P, P], F32, name="stat_t", tag="L")
+        nc.tensor.transpose(stat_t[:], stat[:], ident[:])
+        stat_col = const.tile([P, 1], F32, name="stat_col")
+        nc.vector.tensor_reduce(out=stat_col[:], in_=stat_t[:], axis=AX.X, op=ALU.max)
+        stat_all = ps_l.tile([P, P], F32, name="stat_all", tag="L")
+        nc.tensor.transpose(stat_all[:], stat_col[:, 0:1].to_broadcast([P, P]), ident[:])
+        mxmn = const.tile([P, 2 * D], F32, name="mxmn")
+        nc.vector.tensor_copy(out=mxmn[:], in_=stat_all[:, 0 : 2 * D])
+        span = const.tile([P, D], F32, name="span")
+        nc.vector.tensor_tensor(
+            out=span[:], in0=mxmn[:, 0:D], in1=mxmn[:, D : 2 * D], op=ALU.add
+        )
+        inv = const.tile([P, D], F32, name="inv")
+        nc.vector.reciprocal(inv[:], span[:])
+        xs = const.tile([P, NT, D], F32, name="xs")
+        nc.vector.tensor_tensor(
+            out=xs[:],
+            in0=xb[:],
+            in1=mxmn[:, D : 2 * D].unsqueeze(1).to_broadcast([P, NT, D]),
+            op=ALU.add,
+        )
+        nc.vector.tensor_tensor(
+            out=xs[:], in0=xs[:], in1=inv[:].unsqueeze(1).to_broadcast([P, NT, D]), op=ALU.mult
+        )
+        nhx = const.tile([P, NT, D], F32, name="nhx")
+        nc.vector.tensor_scalar(
+            out=nhx[:], in0=xs[:], scalar1=-0.5, scalar2=None, op0=ALU.mult
+        )
+
+        zf = const.tile([P, PASSES, PACK, D], F32, name="zf")
+        nc.vector.tensor_copy(out=zf[:], in_=zb[:])
+        zt = const.tile([P, D, M], BF16, name="zt")
+        hz = {}
+        cx = {}
+        flip = [0]
+
+        def leave_bank(dst, src):
+            if flip[0] % 2 == 0:
+                nc.scalar.copy(out=dst, in_=src)
+            else:
+                nc.vector.tensor_copy(out=dst, in_=src)
+            flip[0] += 1
+
+        def spread(dst, col_of, dtype, eye):
+            for g in range(PASSES):
+                bank = ps_o.tile([P, PACK, P], dtype, name="bank", tag="O")
+                for t in range(PACK):
+                    nc.tensor.transpose(
+                        bank[:, t, :], col_of(g, t).to_broadcast([P, P]), eye[:]
+                    )
+                leave_bank(
+                    dst[:, g * HALF : (g + 1) * HALF], bank[:].rearrange("p t n -> p (t n)")
+                )
+
+        def spread_dim(d):
+            bank = ps_o.tile([P, PASSES * PACK, P], BF16, name="zbank", tag="O")
+            for g in range(PASSES):
+                for t in range(PACK):
+                    nc.tensor.transpose(
+                        bank[:, PACK * g + t, :],
+                        zb[:, g, t, d : d + 1].to_broadcast([P, P]),
+                        ident_bf[:],
+                    )
+            leave_bank(zt[:, d, :], bank[:].rearrange("p b n -> p (b n)"))
+
+        def spread_half_sums(k):
+            hsum = const.tile([P, PASSES, PACK], F32, name="hsum%d" % k)
+            nc.vector.tensor_reduce(out=hsum[:], in_=zf[:, :, :, 0:k], axis=AX.X, op=ALU.add)
+            hneg = const.tile([P, PASSES, PACK], F32, name="hneg%d" % k)
+            nc.vector.tensor_scalar(
+                out=hneg[:], in0=hsum[:], scalar1=-0.5, scalar2=None, op0=ALU.mult
+            )
+            hz[k] = const.tile([P, M], F32, name="hz%d" % k)
+            spread(hz[k], lambda g, t: hneg[:, g, t : t + 1], F32, ident)
+            cx[k] = const.tile([P, NT], F32, name="cx%d" % k)
+            nc.vector.tensor_reduce(out=cx[k][:], in_=nhx[:, :, 0:k], axis=AX.X, op=ALU.add)
+
+        spread_half_sums(5)
+        for d in (0, 5, 4, 1, 6, 2, 7, 3):
+            spread_dim(d)
+        spread_half_sums(6)
+
+        cgrp = const.tile([P, PASSES, COLS, PACK], BF16, name="cgrp", align_bytes=64)
+        c_codes = const.tile([P, PASSES, COLS], U32, name="c_codes", align_bytes=64)
+        c_scales = const.tile([P, PASSES, COLS], U8, name="c_scales", align_bytes=64)
+
+        def regroup_c(piece):
+            g, h = divmod(piece, 2)
+            cols = slice(h * HALF, (h + 1) * HALF)
+            nc.scalar.copy(
+                out=cgrp[:, g, cols, :].rearrange("p (c i) t -> p c t i", i=4),
+                in_=craw[:, g, :, cols].rearrange("p t (c i) -> p c t i", i=4),
+            )
+
+        def quantise_c(g):
+            nc.vector.quantize_mx(
+                out=c_codes[:, g, :].bitcast(FP8X4),
+                scales=c_scales[:, g, :],
+                in_=cgrp[:, g].rearrange("p c t -> p (c t)"),
+            )
+
+        out_view = out.rearrange("(p j) c -> j p c", j=NT)
+        terms = {}
+        banks = {}
+        groups = {}
+        quant = {}
+        sums = {}
+
+        def stage_terms(j):
+            k = D - n_abs_of(j)
+            n_chain = n_chain_of(j)
+            n_leaf = k - n_chain
+            abs_leaves = []
+            for d in range(k, D):
+                leaf = terms_pool.tile([P, M], F32, name="abs%d" % (d - k))
+                nc.scalar.activation(
+                    out=leaf[:],
+                    in_=zt[:, d, :],
+                    func=ACTF.Abs,
+                    bias=nhx[:, j, d : d + 1],
+                    scale=0.5,
+                )
+                abs_leaves.append(leaf)
+            acc = terms_pool.tile([P, M], F32, name="acc")
+            max_leaves = []
+            for d in range(max(n_chain, n_leaf)):
+                if d == 3 and 0 <= j - 3:
+                    stage_quant(j - 3)
+                if d < n_chain:
+                    nc.vector.scalar_tensor_tensor(
+                        out=acc[:],
+                        in0=zt[:, d, :],
+                        scalar=xs[:, j, d : d + 1],
+                        in1=(hz[k][:] if d == 0 else acc[:]),
+                        op0=ALU.max,
+                        op1=ALU.add,
+                    )
+                if d < n_leaf:
+                    e = n_chain + d
+                    max_leaf = terms_pool.tile([P, M], F32, name="max_leaf%d" % d)
+                    if d == 0:
+                        nc.vector.tensor_scalar(
+                            out=max_leaf[:],
+                            in0=zt[:, e, :],
+                            scalar1=xs[:, j, e : e + 1],
+                            scalar2=cx[k][:, j : j + 1],
+                            op0=ALU.max,
+                            op1=ALU.add,
+                        )
+                    else:
+                        nc.vector.tensor_scalar(
+                            out=max_leaf[:],
+                            in0=zt[:, e, :],
+                            scalar1=xs[:, j, e : e + 1],
+                            scalar2=None,
+                            op0=ALU.max,
+                        )
+                    max_leaves.append(max_leaf)
+            terms[j] = abs_leaves[:1] + max_leaves[:1] + abs_leaves[1:] + max_leaves[1:2] + [acc] + max_leaves[2:]
+
+        def stage_sum(j):
+            made = terms[j]
+            last = len(made) - 1
+            pair = []
+            for g in range(PASSES):
+                bank = ps_l.tile([P, PACK, P], F32, name="l1t", tag="L")
+                pair.append(bank)
+            for i, term in enumerate(made):
+                for g in range(PASSES):
+                    for t in range(PACK):
+                        b = PACK * g + t
+                        nc.tensor.matmul(
+                            pair[g][:, t, :],
+                            lhsT=term[:, b * P : (b + 1) * P],
+                            rhs=ident[:],
+                            is_transpose=True,
+                            start=(i == 0 and t == 0),
+                            stop=(i == last and t == PACK - 1),
+                        )
+            banks[j] = pair
+
+        def stage_exp(j):
+            grp = work.tile([P, PASSES, P, PACK], BF16, name="grp", align_bytes=64)
+            for g, bank in enumerate(banks[j]):
+                nc.scalar.activation(
+                    out=grp[:, g],
+                    in_=bank[:].rearrange("p t n -> p n t"),
+                    func=ACTF.Exp,
+                    scale=-2.0,
+                )
+            groups[j] = grp
+
+        def stage_quant(j):
+            grp = groups[j]
+            codes = work.tile([P, PASSES * P], U32, name="codes", align_bytes=64, bufs=4)
+            scales = work.tile([P, PASSES * P], U8, name="scales", align_bytes=64, bufs=4)
+            nc.vector.quantize_mx(
+                out=codes[:].bitcast(FP8X4),
+                scales=scales[:],
+                in_=grp[:].rearrange("p g n t -> p (g n t)"),
+            )
+            quant[j] = (codes, scales)
+
+        def stage_mx(j):
+            codes, scales = quant[j]
+            sums[j] = []
+            for h in range(COLS // HALF):
+                acc = ps_o.tile([P, HALF], F32, name="osum", tag="O")
+                for g in range(PASSES):
+                    nc.tensor.matmul_mx(
+                        out=acc[:],
+                        lhsT=codes[:, g * P : (g + 1) * P].bitcast(FP8X4),
+                        lhsT_scale=scales[:, g * P : (g + 1) * P],
+                        rhs=c_codes[:, g, h * HALF : (h + 1) * HALF].bitcast(FP8X4),
+                        rhs_scale=c_scales[:, g, h * HALF : (h + 1) * HALF],
+                        start=(g == 0),
+                        stop=(g == PASSES - 1),
+                    )
+                sums[j].append(acc)
+
+        def stage_store(j):
+            res = work.tile([P, COLS], F32, name="res")
+            for h, acc in enumerate(sums[j]):
+                cols = slice(h * HALF, (h + 1) * HALF)
+                if j >= NT - 2 and h == 1:
+                    nc.vector.tensor_copy(out=res[:, cols], in_=acc[:])
+                else:
+                    nc.scalar.copy(out=res[:, cols], in_=acc[:])
+                if j == NT - 1:
+                    nc.sync.dma_start(out=out_view[j][:, cols], in_=res[:, cols])
+            if j < NT - 1:
+                nc.sync.dma_start(out=out_view[j], in_=res[:])
+
+        with tc.manual_schedule():
+            for i in range(NT + 5):
+                if 0 <= i - 3 < NT and not (i < NT and n_chain_of(i) == 4):
+                    stage_quant(i - 3)
+                if 0 <= i - 2 < NT:
+                    stage_exp(i - 2)
+                if 0 <= i - 5 < NT:
+                    stage_store(i - 5)
+                if i < NT:
+                    stage_terms(i)
+                if i == 0:
+                    regroup_c(0)
+                if i < 3:
+                    regroup_c(i + 1)
+                if i == 3:
+                    quantise_c(0)
+                    quantise_c(1)
+                if 0 <= i - 1 < NT:
+                    stage_sum(i - 1)
+                if i % 2 == 0 and 0 <= i - 4 < NT:
+                    stage_mx(i - 4)
+                    stage_mx(i - 3)

@@ -22,16 +22,12 @@ PACK = 4
 PASSES = M // (P * PACK)
 HALF = 512
 FLOPS = 2 * N_ROWS * M * COLS
+FLT_MAX = 3.4028234663852886e38
 
-
-def n_abs_of(j):
-    return 2 if j % 2 == 1 else 3
-
-
-def n_chain_of(j):
-    if j % 2 == 1:
-        return 4
-    return 3 if j % 6 == 0 else 2
+N_CHAIN = 4
+N_POOL = 2
+N_MAX = N_CHAIN + N_POOL
+N_ABS = D - N_MAX
 
 
 def tile_tmgp_sg_kernel(tc, x, design_points, chol_inv, out):
@@ -40,8 +36,9 @@ def tile_tmgp_sg_kernel(tc, x, design_points, chol_inv, out):
         const = ctx.enter_context(tc.tile_pool(name="const", bufs=1))
         terms_pool = ctx.enter_context(tc.tile_pool(name="terms", bufs=4))
         work = ctx.enter_context(tc.tile_pool(name="work", bufs=3))
-        ps_l = ctx.enter_context(tc.psum_pool(name="ps_l", bufs=4))
-        ps_o = ctx.enter_context(tc.psum_pool(name="ps_o", bufs=4))
+        ps_z = ctx.enter_context(tc.psum_pool(name="ps_z", bufs=1))
+        ps_l = ctx.enter_context(tc.psum_pool(name="ps_l", bufs=2))
+        ps_o = ctx.enter_context(tc.psum_pool(name="ps_o", bufs=2))
 
         xb = const.tile([P, NT, D], BF16, name="xb")
         nc.sync.dma_start(out=xb[:], in_=x.rearrange("(p j) d -> p j d", j=NT))
@@ -102,33 +99,22 @@ def tile_tmgp_sg_kernel(tc, x, design_points, chol_inv, out):
             out=nhx[:], in0=xs[:], scalar1=-0.5, scalar2=None, op0=ALU.mult
         )
 
-        zf = const.tile([P, PASSES, PACK, D], F32, name="zf")
-        nc.vector.tensor_copy(out=zf[:], in_=zb[:])
-        zt = const.tile([P, D, M], BF16, name="zt")
-        hz = {}
-        cx = {}
-        flip = [0]
+        zf = const.tile([P, PASSES, PACK, N_MAX], F32, name="zf")
+        nc.vector.tensor_copy(out=zf[:], in_=zb[:, :, :, 0:N_MAX])
+        hsum = const.tile([P, PASSES, PACK], F32, name="hsum")
+        nc.vector.tensor_reduce(out=hsum[:], in_=zf[:], axis=AX.X, op=ALU.add)
+        hneg = const.tile([P, PASSES, PACK], F32, name="hneg")
+        nc.vector.tensor_scalar(
+            out=hneg[:], in0=hsum[:], scalar1=-0.5, scalar2=None, op0=ALU.mult
+        )
+        cx = const.tile([P, NT], F32, name="cx")
+        nc.vector.tensor_reduce(out=cx[:], in_=nhx[:, :, 0:N_MAX], axis=AX.X, op=ALU.add)
 
-        def leave_bank(dst, src):
-            if flip[0] % 2 == 0:
-                nc.scalar.copy(out=dst, in_=src)
-            else:
-                nc.vector.tensor_copy(out=dst, in_=src)
-            flip[0] += 1
+        zt = const.tile([P, D - N_CHAIN, M], BF16, name="zt")
+        hz = const.tile([P, M], F32, name="hz")
+        zp = []
 
-        def spread(dst, col_of, dtype, eye):
-            for g in range(PASSES):
-                bank = ps_o.tile([P, PACK, P], dtype, name="bank", tag="O")
-                for t in range(PACK):
-                    nc.tensor.transpose(
-                        bank[:, t, :], col_of(g, t).to_broadcast([P, P]), eye[:]
-                    )
-                leave_bank(
-                    dst[:, g * HALF : (g + 1) * HALF], bank[:].rearrange("p t n -> p (t n)")
-                )
-
-        def spread_dim(d):
-            bank = ps_o.tile([P, PASSES * PACK, P], BF16, name="zbank", tag="O")
+        def transpose_dim(bank, d):
             for g in range(PASSES):
                 for t in range(PACK):
                     nc.tensor.transpose(
@@ -136,24 +122,37 @@ def tile_tmgp_sg_kernel(tc, x, design_points, chol_inv, out):
                         zb[:, g, t, d : d + 1].to_broadcast([P, P]),
                         ident_bf[:],
                     )
-            leave_bank(zt[:, d, :], bank[:].rearrange("p b n -> p (b n)"))
 
-        def spread_half_sums(k):
-            hsum = const.tile([P, PASSES, PACK], F32, name="hsum%d" % k)
-            nc.vector.tensor_reduce(out=hsum[:], in_=zf[:, :, :, 0:k], axis=AX.X, op=ALU.add)
-            hneg = const.tile([P, PASSES, PACK], F32, name="hneg%d" % k)
-            nc.vector.tensor_scalar(
-                out=hneg[:], in0=hsum[:], scalar1=-0.5, scalar2=None, op0=ALU.mult
-            )
-            hz[k] = const.tile([P, M], F32, name="hz%d" % k)
-            spread(hz[k], lambda g, t: hneg[:, g, t : t + 1], F32, ident)
-            cx[k] = const.tile([P, NT], F32, name="cx%d" % k)
-            nc.vector.tensor_reduce(out=cx[k][:], in_=nhx[:, :, 0:k], axis=AX.X, op=ALU.add)
+        def spread_to_psum(d):
+            bank = ps_z.tile([P, PASSES * PACK, P], BF16, name="zp%d" % d)
+            transpose_dim(bank, d)
+            zp.append(bank[:].rearrange("p b n -> p (b n)"))
 
-        spread_half_sums(5)
-        for d in (0, 5, 4, 1, 6, 2, 7, 3):
-            spread_dim(d)
-        spread_half_sums(6)
+        def spread_to_sbuf(d, copy):
+            bank = ps_o.tile([P, PASSES * PACK, P], BF16, name="zbank", tag="O")
+            transpose_dim(bank, d)
+            copy(out=zt[:, d - N_CHAIN, :], in_=bank[:].rearrange("p b n -> p (b n)"))
+
+        for g in range(PASSES):
+            bank = ps_l.tile([P, PACK, P], F32, name="hbank", tag="L")
+            for t in range(PACK):
+                nc.tensor.transpose(
+                    bank[:, t, :], hneg[:, g, t : t + 1].to_broadcast([P, P]), ident[:]
+                )
+            dst = hz[:, g * HALF : (g + 1) * HALF]
+            src = bank[:].rearrange("p t n -> p (t n)")
+            if g == 0:
+                nc.scalar.copy(out=dst, in_=src)
+            else:
+                nc.vector.tensor_copy(out=dst, in_=src)
+        spread_to_psum(0)
+        spread_to_sbuf(6, nc.scalar.copy)
+        spread_to_sbuf(4, nc.vector.tensor_copy)
+        spread_to_psum(1)
+        spread_to_sbuf(7, nc.scalar.copy)
+        spread_to_sbuf(5, nc.vector.tensor_copy)
+        spread_to_psum(2)
+        spread_to_psum(3)
 
         cgrp = const.tile([P, PASSES, COLS, PACK], BF16, name="cgrp", align_bytes=64)
         c_codes = const.tile([P, PASSES, COLS], U32, name="c_codes", align_bytes=64)
@@ -175,156 +174,157 @@ def tile_tmgp_sg_kernel(tc, x, design_points, chol_inv, out):
             )
 
         out_view = out.rearrange("(p j) c -> j p c", j=NT)
-        terms = {}
+        pool_leaves = {}
+        bases = {}
+        abs_leaves = {}
+        accs = {}
         banks = {}
         groups = {}
         quant = {}
         sums = {}
+        results = {}
 
-        def stage_terms(j):
-            k = D - n_abs_of(j)
-            n_chain = n_chain_of(j)
-            n_leaf = k - n_chain
-            abs_leaves = []
-            for d in range(k, D):
-                leaf = terms_pool.tile([P, M], F32, name="abs%d" % (d - k))
-                nc.scalar.activation(
-                    out=leaf[:],
-                    in_=zt[:, d, :],
-                    func=ACTF.Abs,
-                    bias=nhx[:, j, d : d + 1],
-                    scale=0.5,
+        def pool_terms(j):
+            base = terms_pool.tile([P, M], F32, name="base")
+            nc.gpsimd.tensor_scalar(
+                out=base[:], in0=hz[:], scalar1=1.0, scalar2=cx[:, j : j + 1],
+                op0=ALU.mult, op1=ALU.add,
+            )
+            bases[j] = base
+            pool_leaves[j] = []
+            for d in range(N_CHAIN, N_MAX):
+                leaf = terms_pool.tile([P, M], F32, name="max%d" % d)
+                nc.gpsimd.tensor_scalar(
+                    out=leaf[:], in0=zt[:, d - N_CHAIN, :], scalar1=FLT_MAX,
+                    scalar2=xs[:, j, d : d + 1], op0=ALU.min, op1=ALU.max,
                 )
-                abs_leaves.append(leaf)
-            acc = terms_pool.tile([P, M], F32, name="acc")
-            max_leaves = []
-            for d in range(max(n_chain, n_leaf)):
-                if d == 3 and 0 <= j - 3:
-                    stage_quant(j - 3)
-                if d < n_chain:
-                    nc.vector.scalar_tensor_tensor(
-                        out=acc[:],
-                        in0=zt[:, d, :],
-                        scalar=xs[:, j, d : d + 1],
-                        in1=(hz[k][:] if d == 0 else acc[:]),
-                        op0=ALU.max,
-                        op1=ALU.add,
-                    )
-                if d < n_leaf:
-                    e = n_chain + d
-                    max_leaf = terms_pool.tile([P, M], F32, name="max_leaf%d" % d)
-                    if d == 0:
-                        nc.vector.tensor_scalar(
-                            out=max_leaf[:],
-                            in0=zt[:, e, :],
-                            scalar1=xs[:, j, e : e + 1],
-                            scalar2=cx[k][:, j : j + 1],
-                            op0=ALU.max,
-                            op1=ALU.add,
-                        )
-                    else:
-                        nc.vector.tensor_scalar(
-                            out=max_leaf[:],
-                            in0=zt[:, e, :],
-                            scalar1=xs[:, j, e : e + 1],
-                            scalar2=None,
-                            op0=ALU.max,
-                        )
-                    max_leaves.append(max_leaf)
-            terms[j] = abs_leaves[:1] + max_leaves[:1] + abs_leaves[1:] + max_leaves[1:2] + [acc] + max_leaves[2:]
+                pool_leaves[j].append(leaf)
 
-        def stage_sum(j):
-            made = terms[j]
-            last = len(made) - 1
-            pair = []
+        def abs_term(j, d):
+            leaf = terms_pool.tile([P, M], F32, name="abs%d" % d)
+            nc.scalar.activation(
+                out=leaf[:], in_=zt[:, d - N_CHAIN, :], func=ACTF.Abs,
+                bias=nhx[:, j, d : d + 1], scale=0.5,
+            )
+            abs_leaves.setdefault(j, []).append(leaf)
+
+        def chain_step(j, d):
+            if d == 0:
+                accs[j] = terms_pool.tile([P, M], F32, name="acc")
+            acc = accs[j]
             for g in range(PASSES):
-                bank = ps_l.tile([P, PACK, P], F32, name="l1t", tag="L")
-                pair.append(bank)
-            for i, term in enumerate(made):
-                for g in range(PASSES):
-                    for t in range(PACK):
-                        b = PACK * g + t
-                        nc.tensor.matmul(
-                            pair[g][:, t, :],
-                            lhsT=term[:, b * P : (b + 1) * P],
-                            rhs=ident[:],
-                            is_transpose=True,
-                            start=(i == 0 and t == 0),
-                            stop=(i == last and t == PACK - 1),
-                        )
-            banks[j] = pair
-
-        def stage_exp(j):
-            grp = work.tile([P, PASSES, P, PACK], BF16, name="grp", align_bytes=64)
-            for g, bank in enumerate(banks[j]):
-                nc.scalar.activation(
-                    out=grp[:, g],
-                    in_=bank[:].rearrange("p t n -> p n t"),
-                    func=ACTF.Exp,
-                    scale=-2.0,
+                cols = slice(g * HALF, (g + 1) * HALF)
+                nc.vector.scalar_tensor_tensor(
+                    out=acc[:, cols], in0=zp[d][:, cols], scalar=xs[:, j, d : d + 1],
+                    in1=(bases[j] if d == 0 else acc)[:, cols], op0=ALU.max, op1=ALU.add,
                 )
-            groups[j] = grp
+
+        def stage_sum(j, g):
+            made = abs_leaves[j] + pool_leaves[j] + [accs[j]]
+            last = len(made) - 1
+            bank = ps_l.tile([P, PACK, P], F32, name="l1t", tag="L")
+            banks[j, g] = bank
+            for i, term in enumerate(made):
+                for t in range(PACK):
+                    b = PACK * g + t
+                    nc.tensor.matmul(
+                        bank[:, t, :],
+                        lhsT=term[:, b * P : (b + 1) * P],
+                        rhs=ident[:],
+                        is_transpose=True,
+                        start=(i == 0 and t == 0),
+                        stop=(i == last and t == PACK - 1),
+                    )
+
+        def stage_exp(j, g):
+            if g == 0:
+                groups[j] = work.tile([P, PASSES, P, PACK], BF16, name="grp", align_bytes=64)
+            nc.scalar.activation(
+                out=groups[j][:, g],
+                in_=banks[j, g][:].rearrange("p t n -> p n t"),
+                func=ACTF.Exp,
+                scale=-2.0,
+            )
 
         def stage_quant(j):
-            grp = groups[j]
             codes = work.tile([P, PASSES * P], U32, name="codes", align_bytes=64, bufs=4)
             scales = work.tile([P, PASSES * P], U8, name="scales", align_bytes=64, bufs=4)
             nc.vector.quantize_mx(
                 out=codes[:].bitcast(FP8X4),
                 scales=scales[:],
-                in_=grp[:].rearrange("p g n t -> p (g n t)"),
+                in_=groups[j][:].rearrange("p g n t -> p (g n t)"),
             )
             quant[j] = (codes, scales)
 
-        def stage_mx(j):
-            codes, scales = quant[j]
-            sums[j] = []
-            for h in range(COLS // HALF):
-                acc = ps_o.tile([P, HALF], F32, name="osum", tag="O")
-                for g in range(PASSES):
-                    nc.tensor.matmul_mx(
-                        out=acc[:],
-                        lhsT=codes[:, g * P : (g + 1) * P].bitcast(FP8X4),
-                        lhsT_scale=scales[:, g * P : (g + 1) * P],
-                        rhs=c_codes[:, g, h * HALF : (h + 1) * HALF].bitcast(FP8X4),
-                        rhs_scale=c_scales[:, g, h * HALF : (h + 1) * HALF],
-                        start=(g == 0),
-                        stop=(g == PASSES - 1),
-                    )
-                sums[j].append(acc)
+        def pool_wait(j):
+            token = work.tile([P, 1], U32, name="token")
+            nc.gpsimd.tensor_copy(out=token[:], in_=quant[j][0][:, 0:1])
 
-        def stage_store(j):
-            res = work.tile([P, COLS], F32, name="res")
-            for h, acc in enumerate(sums[j]):
-                cols = slice(h * HALF, (h + 1) * HALF)
-                if j >= NT - 2 and h == 1:
-                    nc.vector.tensor_copy(out=res[:, cols], in_=acc[:])
-                else:
-                    nc.scalar.copy(out=res[:, cols], in_=acc[:])
-                if j == NT - 1:
-                    nc.sync.dma_start(out=out_view[j][:, cols], in_=res[:, cols])
-            if j < NT - 1:
+        def stage_mx(j, h):
+            codes, scales = quant[j]
+            acc = ps_o.tile([P, HALF], F32, name="osum", tag="O")
+            for g in range(PASSES):
+                nc.tensor.matmul_mx(
+                    out=acc[:],
+                    lhsT=codes[:, g * P : (g + 1) * P].bitcast(FP8X4),
+                    lhsT_scale=scales[:, g * P : (g + 1) * P],
+                    rhs=c_codes[:, g, h * HALF : (h + 1) * HALF].bitcast(FP8X4),
+                    rhs_scale=c_scales[:, g, h * HALF : (h + 1) * HALF],
+                    start=(g == 0),
+                    stop=(g == PASSES - 1),
+                )
+            sums[j, h] = acc
+
+        def stage_copy(j, h):
+            if h == 0:
+                results[j] = work.tile([P, COLS], F32, name="res")
+            res = results[j]
+            cols = slice(h * HALF, (h + 1) * HALF)
+            if j >= NT - 3 and h == 1:
+                nc.vector.tensor_copy(out=res[:, cols], in_=sums[j, h][:])
+            else:
+                nc.scalar.copy(out=res[:, cols], in_=sums[j, h][:])
+            if j == NT - 1:
+                nc.sync.dma_start(out=out_view[j][:, cols], in_=res[:, cols])
+            elif h == 1:
                 nc.sync.dma_start(out=out_view[j], in_=res[:])
 
         with tc.manual_schedule():
-            for i in range(NT + 5):
-                if 0 <= i - 3 < NT and not (i < NT and n_chain_of(i) == 4):
-                    stage_quant(i - 3)
-                if 0 <= i - 2 < NT:
-                    stage_exp(i - 2)
-                if 0 <= i - 5 < NT:
-                    stage_store(i - 5)
+            pool_terms(0)
+            for i in range(NT + 4):
+                if 0 <= i - 4 < NT:
+                    stage_copy(i - 4, 1)
                 if i < NT:
-                    stage_terms(i)
+                    abs_term(i, N_MAX)
                 if i == 0:
                     regroup_c(0)
-                if i < 3:
+                    regroup_c(1)
+                if 1 <= i < 3:
                     regroup_c(i + 1)
-                if i == 3:
+                if 0 <= i - 1 < NT:
+                    for g in range(PASSES):
+                        stage_sum(i - 1, g)
+                    stage_exp(i - 1, 0)
+                if i < NT:
+                    abs_term(i, N_MAX + 1)
+                if 0 <= i - 1 < NT:
+                    stage_exp(i - 1, 1)
+                if i < NT:
+                    chain_step(i, 0)
+                    chain_step(i, 1)
+                if 0 <= i - 2 < NT:
+                    stage_quant(i - 2)
+                    if i + 1 < NT:
+                        pool_wait(i - 2)
+                if i + 1 < NT:
+                    pool_terms(i + 1)
+                if i < NT:
+                    chain_step(i, 2)
+                    chain_step(i, 3)
+                if i == 2:
                     quantise_c(0)
                     quantise_c(1)
-                if 0 <= i - 1 < NT:
-                    stage_sum(i - 1)
-                if i % 2 == 0 and 0 <= i - 4 < NT:
-                    stage_mx(i - 4)
-                    stage_mx(i - 3)
+                if 0 <= i - 3 < NT:
+                    stage_mx(i - 3, 0)
+                    stage_mx(i - 3, 1)
+                    stage_copy(i - 3, 0)

@@ -219,22 +219,24 @@ def tile_tmgp_sg_kernel(tc, x, design_points, chol_inv, out):
                     in1=(bases[j] if d == 0 else acc)[:, cols], op0=ALU.max, op1=ALU.add,
                 )
 
-        def stage_sum(j, g):
+        def stage_sum(j):
             made = abs_leaves[j] + pool_leaves[j] + [accs[j]]
             last = len(made) - 1
-            bank = ps_l.tile([P, PACK, P], F32, name="l1t", tag="L")
-            banks[j, g] = bank
+            for g in range(PASSES):
+                bank = ps_l.tile([P, PACK, P], F32, name="l1t", tag="L")
+                banks[j, g] = bank
             for i, term in enumerate(made):
-                for t in range(PACK):
-                    b = PACK * g + t
-                    nc.tensor.matmul(
-                        bank[:, t, :],
-                        lhsT=term[:, b * P : (b + 1) * P],
-                        rhs=ident[:],
-                        is_transpose=True,
-                        start=(i == 0 and t == 0),
-                        stop=(i == last and t == PACK - 1),
-                    )
+                for g in range(PASSES):
+                    for t in range(PACK):
+                        b = PACK * g + t
+                        nc.tensor.matmul(
+                            banks[j, g][:, t, :],
+                            lhsT=term[:, b * P : (b + 1) * P],
+                            rhs=ident[:],
+                            is_transpose=True,
+                            start=(i == 0 and t == 0),
+                            stop=(i == last and t == PACK - 1),
+                        )
 
         def stage_exp(j, g):
             if g == 0:
@@ -291,24 +293,21 @@ def tile_tmgp_sg_kernel(tc, x, design_points, chol_inv, out):
 
         with tc.manual_schedule():
             pool_terms(0)
-            for i in range(NT + 4):
-                if 0 <= i - 4 < NT:
-                    stage_copy(i - 4, 1)
-                if i < NT:
-                    abs_term(i, N_MAX)
-                if i == 0:
-                    regroup_c(0)
-                    regroup_c(1)
-                if 1 <= i < 3:
-                    regroup_c(i + 1)
+            abs_term(0, N_MAX)
+            abs_term(0, N_MAX + 1)
+            for i in range(NT + 3):
                 if 0 <= i - 1 < NT:
-                    for g in range(PASSES):
-                        stage_sum(i - 1, g)
+                    stage_sum(i - 1)
                     stage_exp(i - 1, 0)
-                if i < NT:
-                    abs_term(i, N_MAX + 1)
-                if 0 <= i - 1 < NT:
                     stage_exp(i - 1, 1)
+                if i + 1 < NT:
+                    abs_term(i + 1, N_MAX)
+                    abs_term(i + 1, N_MAX + 1)
+                if 0 <= i - 3 < NT:
+                    stage_mx(i - 3, 0)
+                    stage_mx(i - 3, 1)
+                    stage_copy(i - 3, 0)
+                    stage_copy(i - 3, 1)
                 if i < NT:
                     chain_step(i, 0)
                     chain_step(i, 1)
@@ -321,10 +320,12 @@ def tile_tmgp_sg_kernel(tc, x, design_points, chol_inv, out):
                 if i < NT:
                     chain_step(i, 2)
                     chain_step(i, 3)
+                if i == 0:
+                    regroup_c(0)
+                    regroup_c(1)
+                if i == 1:
+                    regroup_c(2)
+                    regroup_c(3)
                 if i == 2:
                     quantise_c(0)
                     quantise_c(1)
-                if 0 <= i - 3 < NT:
-                    stage_mx(i - 3, 0)
-                    stage_mx(i - 3, 1)
-                    stage_copy(i - 3, 0)

@@ -22,12 +22,33 @@ PACK = 4
 PASSES = M // (P * PACK)
 HALF = 512
 FLOPS = 2 * N_ROWS * M * COLS
+WARM = 4
+RC = 256
+REGROUP = (0, 4, 6, 8)
+CQ = 4
+
+
+MX_START = 4
+EXTRA = (8,)
+
+
+def mx_round():
+    rounds = {}
+    j = 0
+    for i in range(MX_START, NT):
+        n = 2 if i in EXTRA else 1
+        while n > 0 and j <= i - 3:
+            rounds.setdefault(i, []).append(j)
+            j += 1
+            n -= 1
+    return rounds
+
+
 FLT_MAX = 3.4028234663852886e38
 
 N_CHAIN = 4
 N_POOL = 2
 N_MAX = N_CHAIN + N_POOL
-N_ABS = D - N_MAX
 
 
 def tile_tmgp_sg_kernel(tc, x, design_points, chol_inv, out):
@@ -40,127 +61,107 @@ def tile_tmgp_sg_kernel(tc, x, design_points, chol_inv, out):
         ps_l = ctx.enter_context(tc.psum_pool(name="ps_l", bufs=2))
         ps_o = ctx.enter_context(tc.psum_pool(name="ps_o", bufs=2))
 
-        xb = const.tile([P, NT, D], BF16, name="xb")
-        nc.sync.dma_start(out=xb[:], in_=x.rearrange("(p j) d -> p j d", j=NT))
         zb = const.tile([P, PASSES, PACK, D], BF16, name="zb")
-        nc.sync.dma_start(
+        nc.scalar.dma_start(
             out=zb[:],
             in_=design_points.rearrange("(g p t) d -> p g t d", g=PASSES, t=PACK),
         )
+        xb = const.tile([P, NT, D], BF16, name="xb")
+        nc.sync.dma_start(out=xb[:], in_=x.rearrange("(p j) d -> p j d", j=NT))
         craw = const.tile([P, PASSES, PACK, COLS], BF16, name="craw")
         c_view = chol_inv.rearrange("(g p t) c -> g p t c", g=PASSES, t=PACK)
         for g in range(PASSES):
             nc.sync.dma_start(out=craw[:, g], in_=c_view[g])
 
-        ident = const.tile([P, P], F32, name="ident")
-        make_identity(nc, ident[:])
         ident_bf = const.tile([P, P], BF16, name="ident_bf")
         make_identity(nc, ident_bf[:])
-        warm_in = const.tile([P, 1], F32, name="warm_in")
+        ident = const.tile([P, P], F32, name="ident")
+        make_identity(nc, ident[:])
+        warm_in = const.tile([P, HALF], BF16, name="warm_in")
         warm_out = const.tile([P, 1], F32, name="warm_out")
         nc.vector.memset(warm_in[:], 0.0)
-        nc.scalar.activation(out=warm_out[:], in_=warm_in[:], func=ACTF.Exp)
-
-        stat = const.tile([P, P], F32, name="stat")
+        nc.scalar.activation(out=warm_out[:], in_=warm_in[:, 0:1], func=ACTF.Exp)
+        stat = const.tile([P, P], BF16, name="stat")
         nc.vector.memset(stat[:], 0.0)
-        x_by_d = xb[:].rearrange("p j d -> p d j")
-        nc.vector.tensor_reduce(out=stat[:, 0:D], in_=x_by_d, axis=AX.X, op=ALU.max)
-        mn_part = const.tile([P, D], F32, name="mn_part")
-        nc.vector.tensor_reduce(out=mn_part[:], in_=x_by_d, axis=AX.X, op=ALU.min)
-        nc.vector.tensor_scalar(
-            out=stat[:, D : 2 * D], in0=mn_part[:], scalar1=-1.0, scalar2=None, op0=ALU.mult
-        )
-        stat_t = ps_l.tile([P, P], F32, name="stat_t", tag="L")
-        nc.tensor.transpose(stat_t[:], stat[:], ident[:])
-        stat_col = const.tile([P, 1], F32, name="stat_col")
-        nc.vector.tensor_reduce(out=stat_col[:], in_=stat_t[:], axis=AX.X, op=ALU.max)
-        stat_all = ps_l.tile([P, P], F32, name="stat_all", tag="L")
-        nc.tensor.transpose(stat_all[:], stat_col[:, 0:1].to_broadcast([P, P]), ident[:])
-        mxmn = const.tile([P, 2 * D], F32, name="mxmn")
-        nc.vector.tensor_copy(out=mxmn[:], in_=stat_all[:, 0 : 2 * D])
-        span = const.tile([P, D], F32, name="span")
+        pick = const.tile([P, 3 * D], BF16, name="pick")
+        nc.vector.tensor_copy(out=pick[:, 0 : 2 * D], in_=ident_bf[:, 0 : 2 * D])
         nc.vector.tensor_tensor(
-            out=span[:], in0=mxmn[:, 0:D], in1=mxmn[:, D : 2 * D], op=ALU.add
+            out=pick[:, 2 * D : 3 * D], in0=ident_bf[:, 0:D], in1=ident_bf[:, D : 2 * D], op=ALU.add
         )
+        mn_part = const.tile([P, D], BF16, name="mn_part")
+        stat_col = const.tile([P, 1], BF16, name="stat_col")
+        neg_mn = const.tile([P, D], F32, name="neg_mn")
         inv = const.tile([P, D], F32, name="inv")
-        nc.vector.reciprocal(inv[:], span[:])
         xs = const.tile([P, NT, D], F32, name="xs")
-        nc.vector.tensor_tensor(
-            out=xs[:],
-            in0=xb[:],
-            in1=mxmn[:, D : 2 * D].unsqueeze(1).to_broadcast([P, NT, D]),
-            op=ALU.add,
-        )
-        nc.vector.tensor_tensor(
-            out=xs[:], in0=xs[:], in1=inv[:].unsqueeze(1).to_broadcast([P, NT, D]), op=ALU.mult
-        )
         nhx = const.tile([P, NT, D], F32, name="nhx")
-        nc.vector.tensor_scalar(
-            out=nhx[:], in0=xs[:], scalar1=-0.5, scalar2=None, op0=ALU.mult
-        )
-
-        zf = const.tile([P, PASSES, PACK, N_MAX], F32, name="zf")
-        nc.vector.tensor_copy(out=zf[:], in_=zb[:, :, :, 0:N_MAX])
-        hsum = const.tile([P, PASSES, PACK], F32, name="hsum")
-        nc.vector.tensor_reduce(out=hsum[:], in_=zf[:], axis=AX.X, op=ALU.add)
-        hneg = const.tile([P, PASSES, PACK], F32, name="hneg")
-        nc.vector.tensor_scalar(
-            out=hneg[:], in0=hsum[:], scalar1=-0.5, scalar2=None, op0=ALU.mult
-        )
         cx = const.tile([P, NT], F32, name="cx")
-        nc.vector.tensor_reduce(out=cx[:], in_=nhx[:, :, 0:N_MAX], axis=AX.X, op=ALU.add)
-
-        zt = const.tile([P, D - N_CHAIN, M], BF16, name="zt")
+        hsum = const.tile([P, PASSES, PACK], F32, name="hsum")
+        hneg = const.tile([P, PASSES, PACK], F32, name="hneg")
         hz = const.tile([P, M], F32, name="hz")
-        zp = []
+        zt = const.tile([P, D - N_CHAIN, M], BF16, name="zt")
+        zp = {}
 
-        def transpose_dim(bank, d):
+        def warm_up():
+            for n in range(WARM):
+                dummy = ps_o.tile([P, HALF], F32, name="dummy", tag="O")
+                nc.tensor.matmul(
+                    dummy[:], lhsT=warm_in[:, 0:P], rhs=warm_in[:], start=True, stop=True
+                )
+
+        def spread_into(bank, d):
             for g in range(PASSES):
                 for t in range(PACK):
-                    nc.tensor.transpose(
+                    nc.tensor.matmul(
                         bank[:, PACK * g + t, :],
-                        zb[:, g, t, d : d + 1].to_broadcast([P, P]),
-                        ident_bf[:],
+                        lhsT=zb[:, g, t, d : d + 1].to_broadcast([P, P]),
+                        rhs=ident_bf[:],
+                        start=True,
+                        stop=True,
                     )
 
         def spread_to_psum(d):
             bank = ps_z.tile([P, PASSES * PACK, P], BF16, name="zp%d" % d)
-            transpose_dim(bank, d)
-            zp.append(bank[:].rearrange("p b n -> p (b n)"))
+            spread_into(bank, d)
+            zp[d] = bank[:].rearrange("p b n -> p (b n)")
 
         def spread_to_sbuf(d, copy):
             bank = ps_o.tile([P, PASSES * PACK, P], BF16, name="zbank", tag="O")
-            transpose_dim(bank, d)
+            spread_into(bank, d)
             copy(out=zt[:, d - N_CHAIN, :], in_=bank[:].rearrange("p b n -> p (b n)"))
 
-        for g in range(PASSES):
-            bank = ps_l.tile([P, PACK, P], F32, name="hbank", tag="L")
+        def spread_half_sums(g, copy):
+            bank = ps_o.tile([P, PACK, P], F32, name="hbank", tag="O")
             for t in range(PACK):
                 nc.tensor.transpose(
                     bank[:, t, :], hneg[:, g, t : t + 1].to_broadcast([P, P]), ident[:]
                 )
-            dst = hz[:, g * HALF : (g + 1) * HALF]
-            src = bank[:].rearrange("p t n -> p (t n)")
-            if g == 0:
-                nc.scalar.copy(out=dst, in_=src)
-            else:
-                nc.vector.tensor_copy(out=dst, in_=src)
-        spread_to_psum(0)
-        spread_to_sbuf(6, nc.scalar.copy)
-        spread_to_sbuf(4, nc.vector.tensor_copy)
-        spread_to_psum(1)
-        spread_to_sbuf(7, nc.scalar.copy)
-        spread_to_sbuf(5, nc.vector.tensor_copy)
-        spread_to_psum(2)
-        spread_to_psum(3)
+            copy(out=hz[:, g * HALF : (g + 1) * HALF], in_=bank[:].rearrange("p t n -> p (t n)"))
+
+        def scale_rows(a, b, neg_min):
+            nc.vector.tensor_tensor(
+                out=xs[:, a:b],
+                in0=xb[:, a:b],
+                in1=neg_min.unsqueeze(1).to_broadcast([P, b - a, D]),
+                op=ALU.add,
+            )
+            nc.vector.tensor_tensor(
+                out=xs[:, a:b], in0=xs[:, a:b],
+                in1=inv[:].unsqueeze(1).to_broadcast([P, b - a, D]), op=ALU.mult,
+            )
+            nc.vector.tensor_scalar(
+                out=nhx[:, a:b], in0=xs[:, a:b], scalar1=-0.5, scalar2=None, op0=ALU.mult
+            )
+            nc.vector.tensor_reduce(
+                out=cx[:, a:b], in_=nhx[:, a:b, 0:N_MAX], axis=AX.X, op=ALU.add
+            )
 
         cgrp = const.tile([P, PASSES, COLS, PACK], BF16, name="cgrp", align_bytes=64)
         c_codes = const.tile([P, PASSES, COLS], U32, name="c_codes", align_bytes=64)
         c_scales = const.tile([P, PASSES, COLS], U8, name="c_scales", align_bytes=64)
 
         def regroup_c(piece):
-            g, h = divmod(piece, 2)
-            cols = slice(h * HALF, (h + 1) * HALF)
+            g, h = divmod(piece, COLS // RC)
+            cols = slice(h * RC, (h + 1) * RC)
             nc.scalar.copy(
                 out=cgrp[:, g, cols, :].rearrange("p (c i) t -> p c t i", i=4),
                 in_=craw[:, g, :, cols].rearrange("p t (c i) -> p c t i", i=4),
@@ -184,21 +185,26 @@ def tile_tmgp_sg_kernel(tc, x, design_points, chol_inv, out):
         sums = {}
         results = {}
 
-        def pool_terms(j):
+        def base_term(j, engine):
             base = terms_pool.tile([P, M], F32, name="base")
-            nc.gpsimd.tensor_scalar(
+            engine.tensor_scalar(
                 out=base[:], in0=hz[:], scalar1=1.0, scalar2=cx[:, j : j + 1],
                 op0=ALU.mult, op1=ALU.add,
             )
             bases[j] = base
-            pool_leaves[j] = []
-            for d in range(N_CHAIN, N_MAX):
-                leaf = terms_pool.tile([P, M], F32, name="max%d" % d)
-                nc.gpsimd.tensor_scalar(
-                    out=leaf[:], in0=zt[:, d - N_CHAIN, :], scalar1=FLT_MAX,
-                    scalar2=xs[:, j, d : d + 1], op0=ALU.min, op1=ALU.max,
-                )
-                pool_leaves[j].append(leaf)
+
+        def pool_leaf(j, d):
+            leaf = terms_pool.tile([P, M], F32, name="max%d" % d)
+            nc.gpsimd.tensor_scalar(
+                out=leaf[:], in0=zt[:, d - N_CHAIN, :], scalar1=FLT_MAX,
+                scalar2=xs[:, j, d : d + 1], op0=ALU.min, op1=ALU.max,
+            )
+            pool_leaves.setdefault(j, []).append(leaf)
+
+        def pool_terms(j):
+            base_term(j, nc.gpsimd)
+            pool_leaf(j, 4)
+            pool_leaf(j, 5)
 
         def abs_term(j, d):
             leaf = terms_pool.tile([P, M], F32, name="abs%d" % d)
@@ -239,37 +245,53 @@ def tile_tmgp_sg_kernel(tc, x, design_points, chol_inv, out):
                         )
 
         def stage_exp(j, g):
-            if g == 0:
-                groups[j] = work.tile([P, PASSES, P, PACK], BF16, name="grp", align_bytes=64)
+            pair, half = divmod(j, 2)
+            if half == 0 and g == 0:
+                groups[pair] = work.tile([P, 2, PASSES, P, PACK], BF16, name="grp", align_bytes=64)
             nc.scalar.activation(
-                out=groups[j][:, g],
+                out=groups[pair][:, half, g],
                 in_=banks[j, g][:].rearrange("p t n -> p n t"),
                 func=ACTF.Exp,
                 scale=-2.0,
             )
 
-        def stage_quant(j):
-            codes = work.tile([P, PASSES * P], U32, name="codes", align_bytes=64, bufs=4)
-            scales = work.tile([P, PASSES * P], U8, name="scales", align_bytes=64, bufs=4)
+        def stage_quant(pair):
+            codes = work.tile([P, 2 * PASSES * P], U32, name="codes", align_bytes=64)
+            scales = work.tile([P, 2 * PASSES * P], U8, name="scales", align_bytes=64)
             nc.vector.quantize_mx(
                 out=codes[:].bitcast(FP8X4),
                 scales=scales[:],
-                in_=groups[j][:].rearrange("p g n t -> p (g n t)"),
+                in_=groups[pair][:].rearrange("p j g n t -> p (j g n t)"),
             )
-            quant[j] = (codes, scales)
+            quant[pair] = (codes, scales)
 
-        def pool_wait(j):
+        def stage_quant_one(j):
+            pair, half = divmod(j, 2)
+            if half == 0:
+                codes = work.tile([P, 2 * PASSES * P], U32, name="codes", align_bytes=64)
+                scales = work.tile([P, 2 * PASSES * P], U8, name="scales", align_bytes=64)
+                quant[pair] = (codes, scales)
+            codes, scales = quant[pair]
+            cols = slice(half * PASSES * P, (half + 1) * PASSES * P)
+            nc.vector.quantize_mx(
+                out=codes[:, cols].bitcast(FP8X4),
+                scales=scales[:, cols],
+                in_=groups[pair][:, half].rearrange("p g n t -> p (g n t)"),
+            )
+
+        def pool_wait(pair):
             token = work.tile([P, 1], U32, name="token")
-            nc.gpsimd.tensor_copy(out=token[:], in_=quant[j][0][:, 0:1])
+            nc.gpsimd.tensor_copy(out=token[:], in_=quant[pair][0][:, 0:1])
 
-        def stage_mx(j, h):
-            codes, scales = quant[j]
-            acc = ps_o.tile([P, HALF], F32, name="osum", tag="O")
+        def stage_mx(j, h, pool=ps_o, tag="O"):
+            codes, scales = quant[j // 2]
+            acc = pool.tile([P, HALF], F32, name="osum", tag=tag)
             for g in range(PASSES):
+                rows = slice((PASSES * (j % 2) + g) * P, (PASSES * (j % 2) + g + 1) * P)
                 nc.tensor.matmul_mx(
                     out=acc[:],
-                    lhsT=codes[:, g * P : (g + 1) * P].bitcast(FP8X4),
-                    lhsT_scale=scales[:, g * P : (g + 1) * P],
+                    lhsT=codes[:, rows].bitcast(FP8X4),
+                    lhsT_scale=scales[:, rows],
                     rhs=c_codes[:, g, h * HALF : (h + 1) * HALF].bitcast(FP8X4),
                     rhs_scale=c_scales[:, g, h * HALF : (h + 1) * HALF],
                     start=(g == 0),
@@ -291,41 +313,98 @@ def tile_tmgp_sg_kernel(tc, x, design_points, chol_inv, out):
             elif h == 1:
                 nc.sync.dma_start(out=out_view[j], in_=res[:])
 
+        def stage_head():
+            x_by_d = xb[:].rearrange("p j d -> p d j")
+            warm_up()
+            nc.vector.tensor_reduce(out=hsum[:], in_=zb[:, :, :, 0:N_MAX], axis=AX.X, op=ALU.add)
+            nc.vector.tensor_reduce(out=stat[:, 0:D], in_=x_by_d, axis=AX.X, op=ALU.max)
+            nc.vector.tensor_scalar(
+                out=hneg[:], in0=hsum[:], scalar1=-0.5, scalar2=None, op0=ALU.mult
+            )
+            nc.vector.tensor_reduce(out=mn_part[:], in_=x_by_d, axis=AX.X, op=ALU.min)
+            nc.vector.tensor_scalar(
+                out=stat[:, D : 2 * D], in0=mn_part[:], scalar1=-1.0, scalar2=None, op0=ALU.mult
+            )
+            spread_to_psum(0)
+            spread_half_sums(0, nc.scalar.copy)
+            stat_t = ps_l.tile([P, P], BF16, name="stat_t", tag="L")
+            nc.tensor.transpose(stat_t[:], stat[:], ident_bf[:])
+            nc.vector.tensor_reduce(out=stat_col[:], in_=stat_t[:], axis=AX.X, op=ALU.max)
+            spread_half_sums(1, nc.scalar.copy)
+            bank = ps_l.tile([P, 3 * D], F32, name="stat_all", tag="L")
+            nc.tensor.matmul(
+                bank[:], lhsT=stat_col[:, 0:1].to_broadcast([P, P]), rhs=pick[:],
+                start=True, stop=True,
+            )
+            nc.vector.tensor_copy(out=neg_mn[:], in_=bank[:, D : 2 * D])
+            nc.vector.reciprocal(inv[:], bank[:, 2 * D : 3 * D])
+            scale_rows(0, 2, neg_mn[:])
+            spread_to_sbuf(6, nc.scalar.copy)
+            abs_term(0, 6)
+            base_term(0, nc.vector)
+            spread_to_sbuf(4, nc.vector.tensor_copy)
+            pool_leaf(0, 4)
+            spread_to_psum(1)
+            chain_step(0, 0)
+            spread_to_sbuf(7, nc.scalar.copy)
+            abs_term(0, 7)
+            spread_to_sbuf(5, nc.vector.tensor_copy)
+            pool_leaf(0, 5)
+            chain_step(0, 1)
+            spread_to_psum(2)
+            spread_to_psum(3)
+            scale_rows(2, NT, neg_mn[:])
+            pool_terms(1)
+            pool_terms(2)
+            pool_terms(3)
+            chain_step(0, 2)
+            chain_step(0, 3)
+
+        mx_rounds = mx_round()
         with tc.manual_schedule():
-            pool_terms(0)
-            abs_term(0, N_MAX)
-            abs_term(0, N_MAX + 1)
-            for i in range(NT + 3):
-                if 0 <= i - 1 < NT:
+            stage_head()
+            for i in range(NT):
+                if 0 < i:
                     stage_sum(i - 1)
                     stage_exp(i - 1, 0)
                     stage_exp(i - 1, 1)
                 if i + 1 < NT:
-                    abs_term(i + 1, N_MAX)
-                    abs_term(i + 1, N_MAX + 1)
-                if 0 <= i - 3 < NT:
-                    stage_mx(i - 3, 0)
-                    stage_mx(i - 3, 1)
-                    stage_copy(i - 3, 0)
-                    stage_copy(i - 3, 1)
-                if i < NT:
-                    chain_step(i, 0)
-                    chain_step(i, 1)
-                if 0 <= i - 2 < NT:
-                    stage_quant(i - 2)
-                    if i + 1 < NT:
-                        pool_wait(i - 2)
-                if i + 1 < NT:
-                    pool_terms(i + 1)
-                if i < NT:
-                    chain_step(i, 2)
-                    chain_step(i, 3)
-                if i == 0:
-                    regroup_c(0)
-                    regroup_c(1)
-                if i == 1:
-                    regroup_c(2)
-                    regroup_c(3)
-                if i == 2:
+                    abs_term(i + 1, 6)
+                    abs_term(i + 1, 7)
+                if i < len(REGROUP) - 1:
+                    for piece in range(REGROUP[i], REGROUP[i + 1]):
+                        regroup_c(piece)
+                if i == CQ:
                     quantise_c(0)
                     quantise_c(1)
+                if i % 2 == 1 and 0 <= i - 3:
+                    stage_quant((i - 3) // 2)
+                    if i + 2 < NT:
+                        pool_wait((i - 3) // 2)
+                        pool_terms(i + 1)
+                        pool_terms(i + 2)
+                if 0 < i:
+                    for d in range(N_CHAIN):
+                        chain_step(i, d)
+                for j in mx_rounds.get(i, ()):
+                    stage_mx(j, 0)
+                    stage_mx(j, 1)
+                    stage_copy(j, 0)
+                    stage_copy(j, 1)
+            stage_quant_one(NT - 2)
+            stage_sum(NT - 1)
+            stage_exp(NT - 1, 0)
+            stage_exp(NT - 1, 1)
+            stage_mx(NT - 3, 0)
+            stage_mx(NT - 3, 1)
+            stage_quant_one(NT - 1)
+            stage_copy(NT - 3, 0)
+            stage_copy(NT - 3, 1)
+            stage_mx(NT - 2, 0, ps_l, "L")
+            stage_mx(NT - 2, 1, ps_l, "L")
+            stage_copy(NT - 2, 0)
+            stage_copy(NT - 2, 1)
+            stage_mx(NT - 1, 0)
+            stage_mx(NT - 1, 1)
+            stage_copy(NT - 1, 0)
+            stage_copy(NT - 1, 1)

@@ -22,7 +22,7 @@ PACK = 4
 PASSES = M // (P * PACK)
 HALF = 512
 FLOPS = 2 * N_ROWS * M * COLS
-WARM = 4
+WARM = 3
 RC = 256
 REGROUP = (0, 4, 6, 8)
 CQ = 4
@@ -93,7 +93,7 @@ def tile_tmgp_sg_kernel(tc, x, design_points, chol_inv, out):
         neg_mn = const.tile([P, D], F32, name="neg_mn")
         inv = const.tile([P, D], F32, name="inv")
         xs = const.tile([P, NT, D], F32, name="xs")
-        nhx = const.tile([P, NT, D], F32, name="nhx")
+        nhx = const.tile([P, NT, D - N_MAX], F32, name="nhx")
         cx = const.tile([P, NT], F32, name="cx")
         hsum = const.tile([P, PASSES, PACK], F32, name="hsum")
         hneg = const.tile([P, PASSES, PACK], F32, name="hneg")
@@ -137,22 +137,27 @@ def tile_tmgp_sg_kernel(tc, x, design_points, chol_inv, out):
                 )
             copy(out=hz[:, g * HALF : (g + 1) * HALF], in_=bank[:].rearrange("p t n -> p (t n)"))
 
-        def scale_rows(a, b, neg_min):
-            nc.vector.tensor_tensor(
-                out=xs[:, a:b],
-                in0=xb[:, a:b],
-                in1=neg_min.unsqueeze(1).to_broadcast([P, b - a, D]),
-                op=ALU.add,
-            )
-            nc.vector.tensor_tensor(
-                out=xs[:, a:b], in0=xs[:, a:b],
-                in1=inv[:].unsqueeze(1).to_broadcast([P, b - a, D]), op=ALU.mult,
-            )
-            nc.vector.tensor_scalar(
-                out=nhx[:, a:b], in0=xs[:, a:b], scalar1=-0.5, scalar2=None, op0=ALU.mult
-            )
-            nc.vector.tensor_reduce(
-                out=cx[:, a:b], in_=nhx[:, a:b, 0:N_MAX], axis=AX.X, op=ALU.add
+        def scale_rows(a, b):
+            rows = b - a
+            return (
+                lambda: nc.vector.tensor_tensor(
+                    out=xs[:, a:b], in0=xb[:, a:b],
+                    in1=neg_mn[:].unsqueeze(1).to_broadcast([P, rows, D]), op=ALU.add,
+                ),
+                lambda: nc.vector.tensor_tensor(
+                    out=xs[:, a:b], in0=xs[:, a:b],
+                    in1=inv[:].unsqueeze(1).to_broadcast([P, rows, D]), op=ALU.mult,
+                ),
+                lambda: nc.vector.tensor_reduce(
+                    out=cx[:, a:b], in_=xs[:, a:b, 0:N_MAX], axis=AX.X, op=ALU.add
+                ),
+                lambda: nc.vector.tensor_scalar(
+                    out=nhx[:, a:b], in0=xs[:, a:b, N_MAX:D], scalar1=-0.5, scalar2=None,
+                    op0=ALU.mult,
+                ),
+                lambda: nc.vector.tensor_scalar(
+                    out=cx[:, a:b], in0=cx[:, a:b], scalar1=-0.5, scalar2=None, op0=ALU.mult
+                ),
             )
 
         cgrp = const.tile([P, PASSES, COLS, PACK], BF16, name="cgrp", align_bytes=64)
@@ -201,25 +206,21 @@ def tile_tmgp_sg_kernel(tc, x, design_points, chol_inv, out):
             )
             pool_leaves.setdefault(j, []).append(leaf)
 
-        def pool_terms(j):
-            base_term(j, nc.gpsimd)
-            pool_leaf(j, 4)
-            pool_leaf(j, 5)
-
         def abs_term(j, d):
             leaf = terms_pool.tile([P, M], F32, name="abs%d" % d)
             nc.scalar.activation(
                 out=leaf[:], in_=zt[:, d - N_CHAIN, :], func=ACTF.Abs,
-                bias=nhx[:, j, d : d + 1], scale=0.5,
+                bias=nhx[:, j, d - N_MAX : d - N_MAX + 1], scale=0.5,
             )
             abs_leaves.setdefault(j, []).append(leaf)
 
-        def chain_step(j, d):
+        def chain_step(j, d, strands=1):
             if d == 0:
                 accs[j] = terms_pool.tile([P, M], F32, name="acc")
             acc = accs[j]
-            for g in range(PASSES):
-                cols = slice(g * HALF, (g + 1) * HALF)
+            width = M // strands
+            for g in range(strands):
+                cols = slice(g * width, (g + 1) * width)
                 nc.vector.scalar_tensor_tensor(
                     out=acc[:, cols], in0=zp[d][:, cols], scalar=xs[:, j, d : d + 1],
                     in1=(bases[j] if d == 0 else acc)[:, cols], op0=ALU.max, op1=ALU.add,
@@ -338,27 +339,37 @@ def tile_tmgp_sg_kernel(tc, x, design_points, chol_inv, out):
             )
             nc.vector.tensor_copy(out=neg_mn[:], in_=bank[:, D : 2 * D])
             nc.vector.reciprocal(inv[:], bank[:, 2 * D : 3 * D])
-            scale_rows(0, 2, neg_mn[:])
+            for step in scale_rows(0, 2):
+                step()
             spread_to_sbuf(6, nc.scalar.copy)
             abs_term(0, 6)
             base_term(0, nc.vector)
             spread_to_sbuf(4, nc.vector.tensor_copy)
             pool_leaf(0, 4)
             spread_to_psum(1)
-            chain_step(0, 0)
+            rest = scale_rows(2, NT)
+            chain_step(0, 0, 2)
+            rest[0]()
             spread_to_sbuf(7, nc.scalar.copy)
             abs_term(0, 7)
             spread_to_sbuf(5, nc.vector.tensor_copy)
             pool_leaf(0, 5)
-            chain_step(0, 1)
+            rest[1]()
+            chain_step(0, 1, 2)
+            for step in rest[2:4]:
+                step()
             spread_to_psum(2)
             spread_to_psum(3)
-            scale_rows(2, NT, neg_mn[:])
-            pool_terms(1)
-            pool_terms(2)
-            pool_terms(3)
-            chain_step(0, 2)
-            chain_step(0, 3)
+            base_term(1, nc.gpsimd)
+            chain_step(0, 2, 2)
+            rest[4]()
+            base_term(2, nc.gpsimd)
+            for j in range(1, 4):
+                pool_leaf(j, 4)
+                pool_leaf(j, 5)
+                if j < 3:
+                    base_term(j + 2, nc.gpsimd)
+            chain_step(0, 3, 2)
 
         mx_rounds = mx_round()
         with tc.manual_schedule():
@@ -381,11 +392,22 @@ def tile_tmgp_sg_kernel(tc, x, design_points, chol_inv, out):
                     stage_quant((i - 3) // 2)
                     if i + 2 < NT:
                         pool_wait((i - 3) // 2)
-                        pool_terms(i + 1)
-                        pool_terms(i + 2)
-                if 0 < i:
-                    for d in range(N_CHAIN):
-                        chain_step(i, d)
+                    for j in range(i + 1, min(i + 3, NT)):
+                        if j + 1 < NT:
+                            base_term(j + 1, nc.gpsimd)
+                        pool_leaf(j, 4)
+                        pool_leaf(j, 5)
+                if i == 1:
+                    chain_step(1, 0, 2)
+                    chain_step(1, 1, 2)
+                if 0 < i < NT - 1:
+                    chain_step(i + 1, 0)
+                    chain_step(i, 2)
+                    chain_step(i + 1, 1)
+                    chain_step(i, 3)
+                if i == NT - 1:
+                    chain_step(i, 2, 2)
+                    chain_step(i, 3, 2)
                 for j in mx_rounds.get(i, ()):
                     stage_mx(j, 0)
                     stage_mx(j, 1)

@@ -24,12 +24,18 @@ HALF = 512
 FLOPS = 2 * N_ROWS * M * COLS
 WARM = 3
 RC = 256
-REGROUP = (0, 4, 6, 8)
-CQ = 4
+R_PRE = (2, 1)
+R_MID = (3, 2)
+FIRST_WOVEN = 2
+FIRST_SHARED = 5
+SHARE_REST = 3
+ADD_OFF = 0
+CQ0 = 2
+CQ1 = 3
 
 
-MX_START = 4
-EXTRA = (8,)
+MX_START = 3
+EXTRA = ()
 
 
 def mx_round():
@@ -49,6 +55,15 @@ FLT_MAX = 3.4028234663852886e38
 N_CHAIN = 4
 N_POOL = 2
 N_MAX = N_CHAIN + N_POOL
+SHARE = 4
+
+
+def is_shared(j):
+    return j >= FIRST_SHARED and j % SHARE == SHARE_REST
+
+
+def piece_cols(p):
+    return slice(p * M // SHARE, (p + 1) * M // SHARE)
 
 
 def tile_tmgp_sg_kernel(tc, x, design_points, chol_inv, out):
@@ -71,7 +86,9 @@ def tile_tmgp_sg_kernel(tc, x, design_points, chol_inv, out):
         craw = const.tile([P, PASSES, PACK, COLS], BF16, name="craw")
         c_view = chol_inv.rearrange("(g p t) c -> g p t c", g=PASSES, t=PACK)
         for g in range(PASSES):
-            nc.sync.dma_start(out=craw[:, g], in_=c_view[g])
+            for h in range(COLS // HALF):
+                cols = slice(h * HALF, (h + 1) * HALF)
+                nc.sync.dma_start(out=craw[:, g, :, cols], in_=c_view[g][:, :, cols])
 
         ident_bf = const.tile([P, P], BF16, name="ident_bf")
         make_identity(nc, ident_bf[:])
@@ -95,6 +112,8 @@ def tile_tmgp_sg_kernel(tc, x, design_points, chol_inv, out):
         xs = const.tile([P, NT, D], F32, name="xs")
         nhx = const.tile([P, NT, D - N_MAX], F32, name="nhx")
         cx = const.tile([P, NT], F32, name="cx")
+        cx_all = const.tile([P, NT], F32, name="cx_all")
+        row_sum = const.tile([P, NT], F32, name="row_sum")
         hsum = const.tile([P, PASSES, PACK], F32, name="hsum")
         hneg = const.tile([P, PASSES, PACK], F32, name="hneg")
         hz = const.tile([P, M], F32, name="hz")
@@ -149,28 +168,34 @@ def tile_tmgp_sg_kernel(tc, x, design_points, chol_inv, out):
                     in1=inv[:].unsqueeze(1).to_broadcast([P, rows, D]), op=ALU.mult,
                 ),
                 lambda: nc.vector.tensor_reduce(
-                    out=cx[:, a:b], in_=xs[:, a:b, 0:N_MAX], axis=AX.X, op=ALU.add
+                    out=row_sum[:, a:b], in_=xs[:, a:b, 0:N_MAX], axis=AX.X, op=ALU.add
                 ),
                 lambda: nc.vector.tensor_scalar(
                     out=nhx[:, a:b], in0=xs[:, a:b, N_MAX:D], scalar1=-0.5, scalar2=None,
                     op0=ALU.mult,
                 ),
-                lambda: nc.vector.tensor_scalar(
-                    out=cx[:, a:b], in0=cx[:, a:b], scalar1=-0.5, scalar2=None, op0=ALU.mult
-                ),
+            )
+
+        def halve_rows(a, b):
+            nc.vector.tensor_scalar(
+                out=cx[:, a:b], in0=row_sum[:, a:b], scalar1=-0.5, scalar2=None, op0=ALU.mult
             )
 
         cgrp = const.tile([P, PASSES, COLS, PACK], BF16, name="cgrp", align_bytes=64)
         c_codes = const.tile([P, PASSES, COLS], U32, name="c_codes", align_bytes=64)
         c_scales = const.tile([P, PASSES, COLS], U8, name="c_scales", align_bytes=64)
 
-        def regroup_c(piece):
-            g, h = divmod(piece, COLS // RC)
-            cols = slice(h * RC, (h + 1) * RC)
-            nc.scalar.copy(
-                out=cgrp[:, g, cols, :].rearrange("p (c i) t -> p c t i", i=4),
-                in_=craw[:, g, :, cols].rearrange("p t (c i) -> p c t i", i=4),
-            )
+        def regroup_c(n, copy=nc.scalar.copy):
+            for piece in range(done[0], done[0] + n):
+                g, h = divmod(piece, COLS // RC)
+                cols = slice(h * RC, (h + 1) * RC)
+                copy(
+                    out=cgrp[:, g, cols, :].rearrange("p (c i) t -> p c t i", i=4),
+                    in_=craw[:, g, :, cols].rearrange("p t (c i) -> p c t i", i=4),
+                )
+            done[0] += n
+
+        done = [0]
 
         def quantise_c(g):
             nc.vector.quantize_mx(
@@ -193,10 +218,25 @@ def tile_tmgp_sg_kernel(tc, x, design_points, chol_inv, out):
         def base_term(j, engine):
             base = terms_pool.tile([P, M], F32, name="base")
             engine.tensor_scalar(
-                out=base[:], in0=hz[:], scalar1=1.0, scalar2=cx[:, j : j + 1],
+                out=base[:], in0=hz[:], scalar1=1.0,
+                scalar2=cx[:, j : j + 1],
                 op0=ALU.mult, op1=ALU.add,
             )
             bases[j] = base
+
+        def base_piece(j, p):
+            if p == 0:
+                bases[j] = terms_pool.tile([P, M], F32, name="base_s")
+            cols = piece_cols(p)
+            nc.scalar.activation(
+                out=bases[j][:, cols], in_=hz[:, cols], func=ACTF.Identity,
+                bias=cx_all[:, j : j + 1], scale=1.0,
+            )
+
+        def pool_add(j):
+            a, b = pool_leaves[j]
+            nc.gpsimd.tensor_tensor(out=a[:], in0=a[:], in1=b[:], op=ALU.add)
+            pool_leaves[j] = [a]
 
         def pool_leaf(j, d):
             leaf = terms_pool.tile([P, M], F32, name="max%d" % d)
@@ -280,10 +320,6 @@ def tile_tmgp_sg_kernel(tc, x, design_points, chol_inv, out):
                 in_=groups[pair][:, half].rearrange("p g n t -> p (g n t)"),
             )
 
-        def pool_wait(pair):
-            token = work.tile([P, 1], U32, name="token")
-            nc.gpsimd.tensor_copy(out=token[:], in_=quant[pair][0][:, 0:1])
-
         def stage_mx(j, h, pool=ps_o, tag="O"):
             codes, scales = quant[j // 2]
             acc = pool.tile([P, HALF], F32, name="osum", tag=tag)
@@ -341,6 +377,7 @@ def tile_tmgp_sg_kernel(tc, x, design_points, chol_inv, out):
             nc.vector.reciprocal(inv[:], bank[:, 2 * D : 3 * D])
             for step in scale_rows(0, 2):
                 step()
+            halve_rows(0, 2)
             spread_to_sbuf(6, nc.scalar.copy)
             abs_term(0, 6)
             base_term(0, nc.vector)
@@ -362,7 +399,10 @@ def tile_tmgp_sg_kernel(tc, x, design_points, chol_inv, out):
             spread_to_psum(3)
             base_term(1, nc.gpsimd)
             chain_step(0, 2, 2)
-            rest[4]()
+            halve_rows(2, 5)
+            nc.vector.tensor_scalar(
+                out=cx_all[:], in0=row_sum[:], scalar1=-0.5, scalar2=None, op0=ALU.mult
+            )
             base_term(2, nc.gpsimd)
             for j in range(1, 4):
                 pool_leaf(j, 4)
@@ -370,7 +410,6 @@ def tile_tmgp_sg_kernel(tc, x, design_points, chol_inv, out):
                 if j < 3:
                     base_term(j + 2, nc.gpsimd)
             chain_step(0, 3, 2)
-
         mx_rounds = mx_round()
         with tc.manual_schedule():
             stage_head()
@@ -380,27 +419,36 @@ def tile_tmgp_sg_kernel(tc, x, design_points, chol_inv, out):
                     stage_exp(i - 1, 0)
                     stage_exp(i - 1, 1)
                 if i + 1 < NT:
-                    abs_term(i + 1, 6)
+                    regroup_c(R_PRE[i] if i < len(R_PRE) else 0)
                     abs_term(i + 1, 7)
-                if i < len(REGROUP) - 1:
-                    for piece in range(REGROUP[i], REGROUP[i + 1]):
-                        regroup_c(piece)
-                if i == CQ:
+                    abs_term(i + 1, 6)
+                regroup_c(R_MID[i] if i < len(R_MID) else 0)
+                if i == CQ0:
                     quantise_c(0)
+                if i == CQ1:
                     quantise_c(1)
+                for p in range(SHARE):
+                    j = i + SHARE + 1 - p
+                    if j < NT and is_shared(j):
+                        base_piece(j, p)
                 if i % 2 == 1 and 0 <= i - 3:
                     stage_quant((i - 3) // 2)
                     if i + 2 < NT:
-                        pool_wait((i - 3) // 2)
+                        halve_rows(i + 2, min(i + 4, NT))
                     for j in range(i + 1, min(i + 3, NT)):
-                        if j + 1 < NT:
+                        if j + 1 < NT and not is_shared(j + 1):
                             base_term(j + 1, nc.gpsimd)
                         pool_leaf(j, 4)
                         pool_leaf(j, 5)
-                if i == 1:
-                    chain_step(1, 0, 2)
-                    chain_step(1, 1, 2)
-                if 0 < i < NT - 1:
+                        if is_shared(j + ADD_OFF):
+                            pool_add(j)
+                if 0 < i < FIRST_WOVEN:
+                    for d in range(N_CHAIN):
+                        chain_step(i, d, 2)
+                if i == FIRST_WOVEN:
+                    chain_step(i, 0, 2)
+                    chain_step(i, 1, 2)
+                if FIRST_WOVEN <= i < NT - 1:
                     chain_step(i + 1, 0)
                     chain_step(i, 2)
                     chain_step(i + 1, 1)

@@ -26,10 +26,10 @@ WARM = 3
 RC = 256
 R_PRE = (2, 1)
 R_MID = (3, 2)
-FIRST_WOVEN = 2
+FIRST_WOVEN = 1
 FIRST_SHARED = 5
+LAST_ADDS = 1
 SHARE_REST = 3
-ADD_OFF = 0
 CQ0 = 2
 CQ1 = 3
 
@@ -182,8 +182,8 @@ def tile_tmgp_sg_kernel(tc, x, design_points, chol_inv, out):
             )
 
         cgrp = const.tile([P, PASSES, COLS, PACK], BF16, name="cgrp", align_bytes=64)
-        c_codes = const.tile([P, PASSES, COLS], U32, name="c_codes", align_bytes=64)
-        c_scales = const.tile([P, PASSES, COLS], U8, name="c_scales", align_bytes=64)
+        c_codes = const.tile([P, PASSES, COLS], U32, name="c_codes", align_bytes=256)
+        c_scales = const.tile([P, PASSES, COLS], U8, name="c_scales", align_bytes=256)
 
         def regroup_c(n, copy=nc.scalar.copy):
             for piece in range(done[0], done[0] + n):
@@ -233,10 +233,10 @@ def tile_tmgp_sg_kernel(tc, x, design_points, chol_inv, out):
                 bias=cx_all[:, j : j + 1], scale=1.0,
             )
 
-        def pool_add(j):
-            a, b = pool_leaves[j]
-            nc.gpsimd.tensor_tensor(out=a[:], in0=a[:], in1=b[:], op=ALU.add)
-            pool_leaves[j] = [a]
+        def pool_add(j, into, leaves):
+            nc.gpsimd.tensor_tensor(
+                out=into[:], in0=into[:], in1=leaves.pop()[:], op=ALU.add
+            )
 
         def pool_leaf(j, d):
             leaf = terms_pool.tile([P, M], F32, name="max%d" % d)
@@ -297,8 +297,8 @@ def tile_tmgp_sg_kernel(tc, x, design_points, chol_inv, out):
             )
 
         def stage_quant(pair):
-            codes = work.tile([P, 2 * PASSES * P], U32, name="codes", align_bytes=64)
-            scales = work.tile([P, 2 * PASSES * P], U8, name="scales", align_bytes=64)
+            codes = work.tile([P, 2 * PASSES * P], U32, name="codes", align_bytes=256)
+            scales = work.tile([P, 2 * PASSES * P], U8, name="scales", align_bytes=256)
             nc.vector.quantize_mx(
                 out=codes[:].bitcast(FP8X4),
                 scales=scales[:],
@@ -309,8 +309,8 @@ def tile_tmgp_sg_kernel(tc, x, design_points, chol_inv, out):
         def stage_quant_one(j):
             pair, half = divmod(j, 2)
             if half == 0:
-                codes = work.tile([P, 2 * PASSES * P], U32, name="codes", align_bytes=64)
-                scales = work.tile([P, 2 * PASSES * P], U8, name="scales", align_bytes=64)
+                codes = work.tile([P, 2 * PASSES * P], U32, name="codes", align_bytes=256)
+                scales = work.tile([P, 2 * PASSES * P], U8, name="scales", align_bytes=256)
                 quant[pair] = (codes, scales)
             codes, scales = quant[pair]
             cols = slice(half * PASSES * P, (half + 1) * PASSES * P)
@@ -381,7 +381,7 @@ def tile_tmgp_sg_kernel(tc, x, design_points, chol_inv, out):
             spread_to_sbuf(6, nc.scalar.copy)
             abs_term(0, 6)
             base_term(0, nc.vector)
-            spread_to_sbuf(4, nc.vector.tensor_copy)
+            spread_to_sbuf(4, nc.scalar.copy)
             pool_leaf(0, 4)
             spread_to_psum(1)
             rest = scale_rows(2, NT)
@@ -440,8 +440,8 @@ def tile_tmgp_sg_kernel(tc, x, design_points, chol_inv, out):
                             base_term(j + 1, nc.gpsimd)
                         pool_leaf(j, 4)
                         pool_leaf(j, 5)
-                        if is_shared(j + ADD_OFF):
-                            pool_add(j)
+                        if is_shared(j):
+                            pool_add(j, pool_leaves[j][0], pool_leaves[j])
                 if 0 < i < FIRST_WOVEN:
                     for d in range(N_CHAIN):
                         chain_step(i, d, 2)
@@ -461,6 +461,8 @@ def tile_tmgp_sg_kernel(tc, x, design_points, chol_inv, out):
                     stage_mx(j, 1)
                     stage_copy(j, 0)
                     stage_copy(j, 1)
+            for n in range(LAST_ADDS):
+                pool_add(NT - 1, pool_leaves[NT - 1][0], abs_leaves[NT - 1])
             stage_quant_one(NT - 2)
             stage_sum(NT - 1)
             stage_exp(NT - 1, 0)

@@ -59,7 +59,7 @@ SHARE = 4
 
 
 def is_shared(j):
-    return j >= FIRST_SHARED and j % SHARE == SHARE_REST
+    return FIRST_SHARED <= j < NT - 1 and j % SHARE == SHARE_REST
 
 
 def piece_cols(p):
@@ -182,8 +182,8 @@ def tile_tmgp_sg_kernel(tc, x, design_points, chol_inv, out):
             )
 
         cgrp = const.tile([P, PASSES, COLS, PACK], BF16, name="cgrp", align_bytes=64)
-        c_codes = const.tile([P, PASSES, COLS], U32, name="c_codes", align_bytes=256)
-        c_scales = const.tile([P, PASSES, COLS], U8, name="c_scales", align_bytes=256)
+        c_codes = const.tile([P, PASSES, COLS], U32, name="c_codes", align_bytes=64)
+        c_scales = const.tile([P, PASSES, COLS], U8, name="c_scales", align_bytes=64)
 
         def regroup_c(n, copy=nc.scalar.copy):
             for piece in range(done[0], done[0] + n):
@@ -297,8 +297,8 @@ def tile_tmgp_sg_kernel(tc, x, design_points, chol_inv, out):
             )
 
         def stage_quant(pair):
-            codes = work.tile([P, 2 * PASSES * P], U32, name="codes", align_bytes=256)
-            scales = work.tile([P, 2 * PASSES * P], U8, name="scales", align_bytes=256)
+            codes = work.tile([P, 2 * PASSES * P], U32, name="codes", align_bytes=64)
+            scales = work.tile([P, 2 * PASSES * P], U8, name="scales", align_bytes=64)
             nc.vector.quantize_mx(
                 out=codes[:].bitcast(FP8X4),
                 scales=scales[:],
@@ -309,8 +309,8 @@ def tile_tmgp_sg_kernel(tc, x, design_points, chol_inv, out):
         def stage_quant_one(j):
             pair, half = divmod(j, 2)
             if half == 0:
-                codes = work.tile([P, 2 * PASSES * P], U32, name="codes", align_bytes=256)
-                scales = work.tile([P, 2 * PASSES * P], U8, name="scales", align_bytes=256)
+                codes = work.tile([P, 2 * PASSES * P], U32, name="codes", align_bytes=64)
+                scales = work.tile([P, 2 * PASSES * P], U8, name="scales", align_bytes=64)
                 quant[pair] = (codes, scales)
             codes, scales = quant[pair]
             cols = slice(half * PASSES * P, (half + 1) * PASSES * P)
@@ -435,13 +435,12 @@ def tile_tmgp_sg_kernel(tc, x, design_points, chol_inv, out):
                     stage_quant((i - 3) // 2)
                     if i + 2 < NT:
                         halve_rows(i + 2, min(i + 4, NT))
+                    bases_due = [j for j in (i + 2, i + 3) if j < NT and not is_shared(j)]
                     for j in range(i + 1, min(i + 3, NT)):
-                        if j + 1 < NT and not is_shared(j + 1):
-                            base_term(j + 1, nc.gpsimd)
+                        if bases_due:
+                            base_term(bases_due.pop(0), nc.gpsimd)
                         pool_leaf(j, 4)
                         pool_leaf(j, 5)
-                        if is_shared(j):
-                            pool_add(j, pool_leaves[j][0], pool_leaves[j])
                 if 0 < i < FIRST_WOVEN:
                     for d in range(N_CHAIN):
                         chain_step(i, d, 2)

from contextlib import ExitStack

import concourse.mybir as mybir
from concourse.masks import make_identity

F32 = mybir.dt.float32
BF16 = mybir.dt.bfloat16
U32 = mybir.dt.uint32
U8 = mybir.dt.uint8
FP8X4 = mybir.dt.float8_e4m3fn_x4
ALU = mybir.AluOpType
ACTF = mybir.ActivationFunctionType
AX = mybir.AxisListType

P = 128
N_ROWS = 4096
D = 8
M = 1024
COLS = 1024
NT = N_ROWS // P
PACK = 4
PASSES = M // (P * PACK)
HALF = 512
FLOPS = 2 * N_ROWS * M * COLS
WARM = 3
RC = 256
R_PRE = (2, 1)
R_MID = (3, 2)
FIRST_WOVEN = 1
FIRST_SHARED = 5
LAST_ADDS = 1
SHARE_REST = 3
CQ0 = 2
CQ1 = 3


MX_START = 3
EXTRA = ()


def mx_round():
    rounds = {}
    j = 0
    for i in range(MX_START, NT):
        n = 2 if i in EXTRA else 1
        while n > 0 and j <= i - 3:
            rounds.setdefault(i, []).append(j)
            j += 1
            n -= 1
    return rounds


FLT_MAX = 3.4028234663852886e38

N_CHAIN = 4
N_POOL = 2
N_MAX = N_CHAIN + N_POOL
SHARE = 4


def is_shared(j):
    return FIRST_SHARED <= j < NT - 1 and j % SHARE == SHARE_REST


def piece_cols(p):
    return slice(p * M // SHARE, (p + 1) * M // SHARE)


def tile_tmgp_sg_kernel(tc, x, design_points, chol_inv, out):
    nc = tc.nc
    with ExitStack() as ctx:
        const = ctx.enter_context(tc.tile_pool(name="const", bufs=1))
        terms_pool = ctx.enter_context(tc.tile_pool(name="terms", bufs=4))
        work = ctx.enter_context(tc.tile_pool(name="work", bufs=3))
        ps_z = ctx.enter_context(tc.psum_pool(name="ps_z", bufs=1))
        ps_l = ctx.enter_context(tc.psum_pool(name="ps_l", bufs=2))
        ps_o = ctx.enter_context(tc.psum_pool(name="ps_o", bufs=2))

        zb = const.tile([P, PASSES, PACK, D], BF16, name="zb")
        nc.scalar.dma_start(
            out=zb[:],
            in_=design_points.rearrange("(g p t) d -> p g t d", g=PASSES, t=PACK),
        )
        xb = const.tile([P, NT, D], BF16, name="xb")
        nc.sync.dma_start(out=xb[:], in_=x.rearrange("(p j) d -> p j d", j=NT))
        craw = const.tile([P, PASSES, PACK, COLS], BF16, name="craw")
        c_view = chol_inv.rearrange("(g p t) c -> g p t c", g=PASSES, t=PACK)
        for g in range(PASSES):
            for h in range(COLS // HALF):
                cols = slice(h * HALF, (h + 1) * HALF)
                nc.sync.dma_start(out=craw[:, g, :, cols], in_=c_view[g][:, :, cols])

        ident_bf = const.tile([P, P], BF16, name="ident_bf")
        make_identity(nc, ident_bf[:])
        ident = const.tile([P, P], F32, name="ident")
        make_identity(nc, ident[:])
        warm_in = const.tile([P, HALF], BF16, name="warm_in")
        warm_out = const.tile([P, 1], F32, name="warm_out")
        nc.vector.memset(warm_in[:], 0.0)
        nc.scalar.activation(out=warm_out[:], in_=warm_in[:, 0:1], func=ACTF.Exp)
        stat = const.tile([P, P], BF16, name="stat")
        nc.vector.memset(stat[:], 0.0)
        pick = const.tile([P, 3 * D], BF16, name="pick")
        nc.vector.tensor_copy(out=pick[:, 0 : 2 * D], in_=ident_bf[:, 0 : 2 * D])
        nc.vector.tensor_tensor(
            out=pick[:, 2 * D : 3 * D], in0=ident_bf[:, 0:D], in1=ident_bf[:, D : 2 * D], op=ALU.add
        )
        mn_part = const.tile([P, D], BF16, name="mn_part")
        stat_col = const.tile([P, 1], BF16, name="stat_col")
        neg_mn = const.tile([P, D], F32, name="neg_mn")
        inv = const.tile([P, D], F32, name="inv")
        xs = const.tile([P, NT, D], F32, name="xs")
        nhx = const.tile([P, NT, D - N_MAX], F32, name="nhx")
        cx = const.tile([P, NT], F32, name="cx")
        cx_all = const.tile([P, NT], F32, name="cx_all")
        row_sum = const.tile([P, NT], F32, name="row_sum")
        hsum = const.tile([P, PASSES, PACK], F32, name="hsum")
        hneg = const.tile([P, PASSES, PACK], F32, name="hneg")
        hz = const.tile([P, M], F32, name="hz")
        zt = const.tile([P, D - N_CHAIN, M], BF16, name="zt")
        zp = {}

        def warm_up():
            for n in range(WARM):
                dummy = ps_o.tile([P, HALF], F32, name="dummy", tag="O")
                nc.tensor.matmul(
                    dummy[:], lhsT=warm_in[:, 0:P], rhs=warm_in[:], start=True, stop=True
                )

        def spread_into(bank, d):
            for g in range(PASSES):
                for t in range(PACK):
                    nc.tensor.matmul(
                        bank[:, PACK * g + t, :],
                        lhsT=zb[:, g, t, d : d + 1].to_broadcast([P, P]),
                        rhs=ident_bf[:],
                        start=True,
                        stop=True,
                    )

        def spread_to_psum(d):
            bank = ps_z.tile([P, PASSES * PACK, P], BF16, name="zp%d" % d)
            spread_into(bank, d)
            zp[d] = bank[:].rearrange("p b n -> p (b n)")

        def spread_to_sbuf(d, copy):
            bank = ps_o.tile([P, PASSES * PACK, P], BF16, name="zbank", tag="O")
            spread_into(bank, d)
            copy(out=zt[:, d - N_CHAIN, :], in_=bank[:].rearrange("p b n -> p (b n)"))

        def spread_half_sums(g, copy):
            bank = ps_o.tile([P, PACK, P], F32, name="hbank", tag="O")
            for t in range(PACK):
                nc.tensor.transpose(
                    bank[:, t, :], hneg[:, g, t : t + 1].to_broadcast([P, P]), ident[:]
                )
            copy(out=hz[:, g * HALF : (g + 1) * HALF], in_=bank[:].rearrange("p t n -> p (t n)"))

        def scale_rows(a, b):
            rows = b - a
            return (
                lambda: nc.vector.tensor_tensor(
                    out=xs[:, a:b], in0=xb[:, a:b],
                    in1=neg_mn[:].unsqueeze(1).to_broadcast([P, rows, D]), op=ALU.add,
                ),
                lambda: nc.vector.tensor_tensor(
                    out=xs[:, a:b], in0=xs[:, a:b],
                    in1=inv[:].unsqueeze(1).to_broadcast([P, rows, D]), op=ALU.mult,
                ),
                lambda: nc.vector.tensor_reduce(
                    out=row_sum[:, a:b], in_=xs[:, a:b, 0:N_MAX], axis=AX.X, op=ALU.add
                ),
                lambda: nc.vector.tensor_scalar(
                    out=nhx[:, a:b], in0=xs[:, a:b, N_MAX:D], scalar1=-0.5, scalar2=None,
                    op0=ALU.mult,
                ),
            )

        def halve_rows(a, b):
            nc.vector.tensor_scalar(
                out=cx[:, a:b], in0=row_sum[:, a:b], scalar1=-0.5, scalar2=None, op0=ALU.mult
            )

        cgrp = const.tile([P, PASSES, COLS, PACK], BF16, name="cgrp", align_bytes=64)
        c_codes = const.tile([P, PASSES, COLS], U32, name="c_codes", align_bytes=64)
        c_scales = const.tile([P, PASSES, COLS], U8, name="c_scales", align_bytes=64)

        def regroup_c(n, copy=nc.scalar.copy):
            for piece in range(done[0], done[0] + n):
                g, h = divmod(piece, COLS // RC)
                cols = slice(h * RC, (h + 1) * RC)
                copy(
                    out=cgrp[:, g, cols, :].rearrange("p (c i) t -> p c t i", i=4),
                    in_=craw[:, g, :, cols].rearrange("p t (c i) -> p c t i", i=4),
                )
            done[0] += n

        done = [0]

        def quantise_c(g):
            nc.vector.quantize_mx(
                out=c_codes[:, g, :].bitcast(FP8X4),
                scales=c_scales[:, g, :],
                in_=cgrp[:, g].rearrange("p c t -> p (c t)"),
            )

        out_view = out.rearrange("(p j) c -> j p c", j=NT)
        pool_leaves = {}
        bases = {}
        abs_leaves = {}
        accs = {}
        banks = {}
        groups = {}
        quant = {}
        sums = {}
        results = {}

        def base_term(j, engine):
            base = terms_pool.tile([P, M], F32, name="base")
            engine.tensor_scalar(
                out=base[:], in0=hz[:], scalar1=1.0,
                scalar2=cx[:, j : j + 1],
                op0=ALU.mult, op1=ALU.add,
            )
            bases[j] = base

        def base_piece(j, p):
            if p == 0:
                bases[j] = terms_pool.tile([P, M], F32, name="base_s")
            cols = piece_cols(p)
            nc.scalar.activation(
                out=bases[j][:, cols], in_=hz[:, cols], func=ACTF.Identity,
                bias=cx_all[:, j : j + 1], scale=1.0,
            )

        def pool_add(j, into, leaves):
            nc.gpsimd.tensor_tensor(
                out=into[:], in0=into[:], in1=leaves.pop()[:], op=ALU.add
            )

        def pool_leaf(j, d):
            leaf = terms_pool.tile([P, M], F32, name="max%d" % d)
            nc.gpsimd.tensor_scalar(
                out=leaf[:], in0=zt[:, d - N_CHAIN, :], scalar1=FLT_MAX,
                scalar2=xs[:, j, d : d + 1], op0=ALU.min, op1=ALU.max,
            )
            pool_leaves.setdefault(j, []).append(leaf)

        def abs_term(j, d):
            leaf = terms_pool.tile([P, M], F32, name="abs%d" % d)
            nc.scalar.activation(
                out=leaf[:], in_=zt[:, d - N_CHAIN, :], func=ACTF.Abs,
                bias=nhx[:, j, d - N_MAX : d - N_MAX + 1], scale=0.5,
            )
            abs_leaves.setdefault(j, []).append(leaf)

        def chain_step(j, d, strands=1):
            if d == 0:
                accs[j] = terms_pool.tile([P, M], F32, name="acc")
            acc = accs[j]
            width = M // strands
            for g in range(strands):
                cols = slice(g * width, (g + 1) * width)
                nc.vector.scalar_tensor_tensor(
                    out=acc[:, cols], in0=zp[d][:, cols], scalar=xs[:, j, d : d + 1],
                    in1=(bases[j] if d == 0 else acc)[:, cols], op0=ALU.max, op1=ALU.add,
                )

        def stage_sum(j):
            made = abs_leaves[j] + pool_leaves[j] + [accs[j]]
            last = len(made) - 1
            for g in range(PASSES):
                bank = ps_l.tile([P, PACK, P], F32, name="l1t", tag="L")
                banks[j, g] = bank
            for i, term in enumerate(made):
                for g in range(PASSES):
                    for t in range(PACK):
                        b = PACK * g + t
                        nc.tensor.matmul(
                            banks[j, g][:, t, :],
                            lhsT=term[:, b * P : (b + 1) * P],
                            rhs=ident[:],
                            is_transpose=True,
                            start=(i == 0 and t == 0),
                            stop=(i == last and t == PACK - 1),
                        )

        def stage_exp(j, g):
            pair, half = divmod(j, 2)
            if half == 0 and g == 0:
                groups[pair] = work.tile([P, 2, PASSES, P, PACK], BF16, name="grp", align_bytes=64)
            nc.scalar.activation(
                out=groups[pair][:, half, g],
                in_=banks[j, g][:].rearrange("p t n -> p n t"),
                func=ACTF.Exp,
                scale=-2.0,
            )

        def stage_quant(pair):
            codes = work.tile([P, 2 * PASSES * P], U32, name="codes", align_bytes=64)
            scales = work.tile([P, 2 * PASSES * P], U8, name="scales", align_bytes=64)
            nc.vector.quantize_mx(
                out=codes[:].bitcast(FP8X4),
                scales=scales[:],
                in_=groups[pair][:].rearrange("p j g n t -> p (j g n t)"),
            )
            quant[pair] = (codes, scales)

        def stage_quant_one(j):
            pair, half = divmod(j, 2)
            if half == 0:
                codes = work.tile([P, 2 * PASSES * P], U32, name="codes", align_bytes=64)
                scales = work.tile([P, 2 * PASSES * P], U8, name="scales", align_bytes=64)
                quant[pair] = (codes, scales)
            codes, scales = quant[pair]
            cols = slice(half * PASSES * P, (half + 1) * PASSES * P)
            nc.vector.quantize_mx(
                out=codes[:, cols].bitcast(FP8X4),
                scales=scales[:, cols],
                in_=groups[pair][:, half].rearrange("p g n t -> p (g n t)"),
            )

        def stage_mx(j, h, pool=ps_o, tag="O"):
            codes, scales = quant[j // 2]
            acc = pool.tile([P, HALF], F32, name="osum", tag=tag)
            for g in range(PASSES):
                rows = slice((PASSES * (j % 2) + g) * P, (PASSES * (j % 2) + g + 1) * P)
                nc.tensor.matmul_mx(
                    out=acc[:],
                    lhsT=codes[:, rows].bitcast(FP8X4),
                    lhsT_scale=scales[:, rows],
                    rhs=c_codes[:, g, h * HALF : (h + 1) * HALF].bitcast(FP8X4),
                    rhs_scale=c_scales[:, g, h * HALF : (h + 1) * HALF],
                    start=(g == 0),
                    stop=(g == PASSES - 1),
                )
            sums[j, h] = acc

        def stage_copy(j, h):
            if h == 0:
                results[j] = work.tile([P, COLS], F32, name="res")
            res = results[j]
            cols = slice(h * HALF, (h + 1) * HALF)
            if j >= NT - 3 and h == 1:
                nc.vector.tensor_copy(out=res[:, cols], in_=sums[j, h][:])
            else:
                nc.scalar.copy(out=res[:, cols], in_=sums[j, h][:])
            if j == NT - 1:
                nc.sync.dma_start(out=out_view[j][:, cols], in_=res[:, cols])
            elif h == 1:
                nc.sync.dma_start(out=out_view[j], in_=res[:])

        def stage_head():
            x_by_d = xb[:].rearrange("p j d -> p d j")
            warm_up()
            nc.vector.tensor_reduce(out=hsum[:], in_=zb[:, :, :, 0:N_MAX], axis=AX.X, op=ALU.add)
            nc.vector.tensor_reduce(out=stat[:, 0:D], in_=x_by_d, axis=AX.X, op=ALU.max)
            nc.vector.tensor_scalar(
                out=hneg[:], in0=hsum[:], scalar1=-0.5, scalar2=None, op0=ALU.mult
            )
            nc.vector.tensor_reduce(out=mn_part[:], in_=x_by_d, axis=AX.X, op=ALU.min)
            nc.vector.tensor_scalar(
                out=stat[:, D : 2 * D], in0=mn_part[:], scalar1=-1.0, scalar2=None, op0=ALU.mult
            )
            spread_to_psum(0)
            spread_half_sums(0, nc.scalar.copy)
            stat_t = ps_l.tile([P, P], BF16, name="stat_t", tag="L")
            nc.tensor.transpose(stat_t[:], stat[:], ident_bf[:])
            nc.vector.tensor_reduce(out=stat_col[:], in_=stat_t[:], axis=AX.X, op=ALU.max)
            spread_half_sums(1, nc.scalar.copy)
            bank = ps_l.tile([P, 3 * D], F32, name="stat_all", tag="L")
            nc.tensor.matmul(
                bank[:], lhsT=stat_col[:, 0:1].to_broadcast([P, P]), rhs=pick[:],
                start=True, stop=True,
            )
            nc.vector.tensor_copy(out=neg_mn[:], in_=bank[:, D : 2 * D])
            nc.vector.reciprocal(inv[:], bank[:, 2 * D : 3 * D])
            for step in scale_rows(0, 2):
                step()
            halve_rows(0, 2)
            spread_to_sbuf(6, nc.scalar.copy)
            abs_term(0, 6)
            base_term(0, nc.vector)
            spread_to_sbuf(4, nc.scalar.copy)
            pool_leaf(0, 4)
            spread_to_psum(1)
            rest = scale_rows(2, NT)
            chain_step(0, 0, 2)
            rest[0]()
            spread_to_sbuf(7, nc.scalar.copy)
            abs_term(0, 7)
            spread_to_sbuf(5, nc.vector.tensor_copy)
            pool_leaf(0, 5)
            rest[1]()
            chain_step(0, 1, 2)
            for step in rest[2:4]:
                step()
            spread_to_psum(2)
            spread_to_psum(3)
            base_term(1, nc.gpsimd)
            chain_step(0, 2, 2)
            halve_rows(2, 5)
            nc.vector.tensor_scalar(
                out=cx_all[:], in0=row_sum[:], scalar1=-0.5, scalar2=None, op0=ALU.mult
            )
            base_term(2, nc.gpsimd)
            for j in range(1, 4):
                pool_leaf(j, 4)
                pool_leaf(j, 5)
                if j < 3:
                    base_term(j + 2, nc.gpsimd)
            chain_step(0, 3, 2)
        mx_rounds = mx_round()
        with tc.manual_schedule():
            stage_head()
            for i in range(NT):
                if 0 < i:
                    stage_sum(i - 1)
                    stage_exp(i - 1, 0)
                    stage_exp(i - 1, 1)
                if i + 1 < NT:
                    regroup_c(R_PRE[i] if i < len(R_PRE) else 0)
                    abs_term(i + 1, 7)
                    abs_term(i + 1, 6)
                regroup_c(R_MID[i] if i < len(R_MID) else 0)
                if i == CQ0:
                    quantise_c(0)
                if i == CQ1:
                    quantise_c(1)
                for p in range(SHARE):
                    j = i + SHARE + 1 - p
                    if j < NT and is_shared(j):
                        base_piece(j, p)
                if i % 2 == 1 and 0 <= i - 3:
                    stage_quant((i - 3) // 2)
                    if i + 2 < NT:
                        halve_rows(i + 2, min(i + 4, NT))
                    bases_due = [j for j in (i + 2, i + 3) if j < NT and not is_shared(j)]
                    for j in range(i + 1, min(i + 3, NT)):
                        if bases_due:
                            base_term(bases_due.pop(0), nc.gpsimd)
                        pool_leaf(j, 4)
                        pool_leaf(j, 5)
                if 0 < i < FIRST_WOVEN:
                    for d in range(N_CHAIN):
                        chain_step(i, d, 2)
                if i == FIRST_WOVEN:
                    chain_step(i, 0, 2)
                    chain_step(i, 1, 2)
                if FIRST_WOVEN <= i < NT - 1:
                    chain_step(i + 1, 0)
                    chain_step(i, 2)
                    chain_step(i + 1, 1)
                    chain_step(i, 3)
                if i == NT - 1:
                    chain_step(i, 2, 2)
                    chain_step(i, 3, 2)
                for j in mx_rounds.get(i, ()):
                    stage_mx(j, 0)
                    stage_mx(j, 1)
                    stage_copy(j, 0)
                    stage_copy(j, 1)
            for n in range(LAST_ADDS):
                pool_add(NT - 1, pool_leaves[NT - 1][0], abs_leaves[NT - 1])
            stage_quant_one(NT - 2)
            stage_sum(NT - 1)
            stage_exp(NT - 1, 0)
            stage_exp(NT - 1, 1)
            stage_mx(NT - 3, 0)
            stage_mx(NT - 3, 1)
            stage_quant_one(NT - 1)
            stage_copy(NT - 3, 0)
            stage_copy(NT - 3, 1)
            stage_mx(NT - 2, 0, ps_l, "L")
            stage_mx(NT - 2, 1, ps_l, "L")
            stage_copy(NT - 2, 0)
            stage_copy(NT - 2, 1)
            stage_mx(NT - 1, 0)
            stage_mx(NT - 1, 1)
            stage_copy(NT - 1, 0)
            stage_copy(NT - 1, 1)
